import numpy as np
import ml_dtypes


def mxq(x, axis, fmt="e4m3"):
    dtype, down = {"e4m3": (ml_dtypes.float8_e4m3fn, 7), "e5m2": (ml_dtypes.float8_e5m2, 14)}[fmt]
    v = np.moveaxis(np.asarray(x, np.float32).astype(ml_dtypes.bfloat16).astype(np.float64), axis, -1)
    blocks = v.reshape(v.shape[:-1] + (-1, 32))
    amax = np.abs(blocks).max(-1, keepdims=True)
    byte = np.maximum(np.where(amax > 0, np.frexp(amax)[1] - 1 + 127, 0) - down, 1)
    scale = np.exp2(byte - 127.0)
    codes = (blocks / scale).astype(np.float32).astype(dtype).astype(np.float64)
    return np.moveaxis((codes * scale).reshape(v.shape), -1, axis)


WIDE = False


def mx_kscale(k):
    if not WIDE:
        return np.ones(k)
    levels = np.array([10, -10, 5, -5, 0])
    if k % 512:
        return np.exp2(np.random.permutation(np.resize(levels, k // 32))).repeat(32)
    a = np.empty((k // 512, 16))
    for p in range(k // 512):
        a[p, :8] = np.random.permutation(np.resize(levels, 8))
        for g in range(8):
            far = levels[np.abs(levels - a[p, g]) >= 10]
            a[p, g + 8] = far[np.random.randint(len(far))]
    return np.exp2(a.ravel()).repeat(32)


BF16 = ml_dtypes.bfloat16


def bf(x):
    return np.asarray(x, np.float32).astype(BF16)


def f64(x):
    return np.asarray(x).astype(np.float64)


B, S, D_MODEL, N_HEADS, QK_ROPE, QK_NOPE, KV_LORA, V_DIM = 2, 1024, 8192, 16, 128, 128, 2048, 128
RMS_EPS = 1.1920928955078125e-07
ROPE_BASE = 10000.0


def apply_rope(r):
    freqs = 1.0 / (ROPE_BASE ** (np.arange(0, QK_ROPE, 2) / QK_ROPE))
    t = np.arange(S)[:, None] * freqs[None, :]
    cos = np.cos(t)[None, :, None, :]
    sin = np.sin(t)[None, :, None, :]
    r1 = r[..., 0::2]
    r2 = r[..., 1::2]
    return np.stack([r1 * cos - r2 * sin, r2 * cos + r1 * sin], axis=-1).reshape(r.shape)


def setup_inputs():
    s, t = mx_kscale(D_MODEL), mx_kscale(KV_LORA)
    return {"x": bf(np.random.standard_normal((B, S, D_MODEL)) * s),
            "Wkv_a": bf(np.random.standard_normal((D_MODEL, KV_LORA + QK_ROPE)) / np.sqrt(D_MODEL) / s[:, None]),
            "kv_norm_w": bf((1.0 + 0.1 * np.random.standard_normal(KV_LORA)) * t),
            "Wkv_b": bf(np.random.standard_normal((KV_LORA, N_HEADS * (QK_NOPE + V_DIM))) / np.sqrt(KV_LORA) / t[:, None])}


def reference(x, Wkv_a, kv_norm_w, Wkv_b):
    kv = mxq(f64(x), 2, "e4m3") @ mxq(f64(Wkv_a), 0, "e4m3")
    c_kv, k_rope = kv[..., :KV_LORA], kv[..., KV_LORA:]
    k_rope = apply_rope(k_rope.reshape(B, S, 1, QK_ROPE))
    c_kv = c_kv * (1.0 / np.sqrt(np.mean(c_kv * c_kv, axis=-1, keepdims=True) + RMS_EPS)) * f64(kv_norm_w)
    kv = (mxq(c_kv, 2, "e4m3") @ mxq(f64(Wkv_b), 0, "e4m3")).reshape(B, S, N_HEADS, QK_NOPE + V_DIM)
    return kv[..., :QK_NOPE], kv[..., QK_NOPE:], k_rope

@@ -1,0 +1,430 @@
+from contextlib import ExitStack
+import math
+
+import concourse.masks as masks
+import concourse.mybir as mybir
+
+FLOPS = 2 * 2048 * 8192 * 2176 + 2 * 2048 * 2048 * 4096
+
+F32 = mybir.dt.float32
+BF16 = mybir.dt.bfloat16
+U32 = mybir.dt.uint32
+U8 = mybir.dt.uint8
+I32 = mybir.dt.int32
+FP8X4 = mybir.dt.float8_e4m3fn_x4
+ALU = mybir.AluOpType
+ACT = mybir.ActivationFunctionType
+AX = mybir.AxisListType
+
+P = 128
+NT = 16
+G1 = 16
+G2 = 4
+CW = 256
+NCH = 8
+EPS = 1.1920928955078125e-07
+TWO_PI = 6.283185307179586
+
+XC0 = 0
+XS0 = XC0 + 16 * 8192
+WC0 = XS0 + 16 * 512
+WS0 = WC0 + 2 * 16384
+WR0 = WS0 + 2 * 1024
+RC0 = WR0 + 3 * 4096
+RS0 = RC0 + 8192
+CF0 = RS0 + 512
+SF0 = CF0 + 4096
+WG0 = SF0 + 4096
+XR0 = WG0 + 2 * 4096
+XG0 = XR0 + 3 * 4096
+CS0 = XG0 + 2 * 4096
+GN0 = CS0 + 3 * 2048
+ID0 = GN0 + 4096
+SQ0 = ID0 + 512
+JK0 = SQ0 + 512
+SM0 = JK0 + 512
+CB_OFF = (WR0, WR0 + 8192, XC0, XC0 + 8192)
+NB_OFF = (WR0 + 16384, WR0 + 20480)
+NG_OFF = (WR0 + 24576, CS0)
+NC0 = XC0 + 2 * 8192
+WBR0 = WC0
+WBC_OFF = (XR0, XC0 + 6 * 8192)
+OS0 = XC0 + 9 * 8192
+
+
+def split3(c):
+    e = -int(-math.log(c) / math.log(2.0)) - 1
+    s1 = 2.0 ** (11 - e)
+    hi = int(c * s1) / s1
+    s2 = s1 * 4194304.0
+    mid = int((c - hi) * s2) / s2
+    lo = (c - hi) - mid
+    return hi, mid, lo
+
+
+def tile_multiheadlatentattention_pa_l_kernel(tc, x, Wkv_a, kv_norm_w, Wkv_b, out_0, out_1, out_2):
+    nc = tc.nc
+    xf = x.flatten_outer_dims()
+    o_k = out_0.rearrange("b s h d -> (b s) (h d)")
+    o_v = out_1.rearrange("b s h d -> (b s) (h d)")
+    o_r = out_2.rearrange("b s o d -> (b s) (o d)")
+
+    with ExitStack() as ctx:
+        sb = ctx.enter_context(tc.tile_pool(name="sb", bufs=1))
+        ps = ctx.enter_context(tc.psum_pool(name="ps", bufs=8))
+        cnt = {"wr": 0, "wg": 0, "xr": 0, "xg": 0, "cs": 0, "wbr": 0, "nb": 0, "ng": 0, "os": 0}
+
+        def st(shape, dtype, tag, offset):
+            return sb.tile(shape, dtype, name=tag, tag=tag, offset=offset, align_bytes=64)
+
+        def ring(kind, shape, dtype, base, size, depth):
+            n = cnt[kind] % depth
+            cnt[kind] = cnt[kind] + 1
+            return st(shape, dtype, "%s%d" % (kind, n), base + size * n)
+
+        def ring_at(kind, shape, dtype, offsets):
+            n = cnt[kind] % len(offsets)
+            cnt[kind] = cnt[kind] + 1
+            return st(shape, dtype, "%s%d" % (kind, n), offsets[n])
+
+        def bank():
+            return ps.tile([P, 512], F32, name="bank", tag="bank")
+
+        ident = st([P, P], F32, "ident", ID0)
+        masks.make_identity(nc, ident[:])
+        ssq = st([P, NT * NCH], F32, "ssq", SQ0)
+        junk = st([P, CW], BF16, "junk", JK0)
+        neghalf = st([P, 2], F32, "neghalf", SM0)
+        nc.vector.memset(neghalf[:], -0.5)
+        gain = st([P, 2048], BF16, "gain", GN0)
+
+        xc = {}
+        xs = {}
+        wch = {}
+
+        def turn(src, dst, copy):
+            words = src[:].bitcast(F32)
+            dstw = dst[:].bitcast(F32)
+            for hb in range(2):
+                bk = bank()
+                for l in range(2):
+                    for u in range(2):
+                        lo = 256 * (2 * hb + l)
+                        nc.tensor.transpose(
+                            bk[:, 256 * l + 128 * u : 256 * l + 128 * (u + 1)],
+                            words[:, lo + u : lo + 256 : 2],
+                            ident[:],
+                        )
+                copy(
+                    out=dstw[:, 512 * hb : 512 * (hb + 1)].rearrange("p (l m u) -> p l m u", l=2, u=2),
+                    in_=bk[:].rearrange("p (l u m) -> p l m u", l=2, u=2),
+                )
+
+        def x_unit(i, q):
+            xr = ring("xr", [P, 2048], BF16, XR0, 4096, 3)
+            nc.sync.dma_start(out=xr[:], in_=xf[128 * i : 128 * (i + 1), 2048 * q : 2048 * (q + 1)])
+            xg = ring("xg", [P, 2048], BF16, XG0, 4096, 2)
+            turn(xr, xg, nc.scalar.copy)
+            nc.vector.quantize_mx(
+                out=xc[i][:, 512 * q : 512 * (q + 1)].bitcast(FP8X4),
+                scales=xs[i][4 * q : 128, :],
+                in_=xg[:],
+            )
+
+        def wa_unit(j, s):
+            if s == 0:
+                wch[j] = (
+                    st([P, G1 * CW], U32, "wc%d" % (j % 2), WC0 + 16384 * (j % 2)),
+                    st([P, 4 * CW], U8, "ws%d" % (j % 2), WS0 + 1024 * (j % 2)),
+                )
+            wc, ws = wch[j]
+            wr = ring("wr", [P, 2, 4, CW], BF16, WR0, 4096, 3)
+            for l in range(2):
+                g = 2 * s + l
+                nc.sync.dma_start(
+                    out=wr[:, l, :, :],
+                    in_=Wkv_a[512 * g : 512 * (g + 1), CW * j : CW * (j + 1)].rearrange("(p t) c -> p t c", t=4),
+                )
+            wg = ring("wg", [P, 2048], BF16, WG0, 4096, 2)
+            nc.vector.tensor_copy(
+                out=wg[:].rearrange("p (l c t) -> p l c t", l=2, t=4),
+                in_=wr[:].rearrange("p l t c -> p l c t"),
+            )
+            q, r = divmod(2 * s, 4)
+            nc.vector.quantize_mx(
+                out=wc[:, 512 * s : 512 * (s + 1)].bitcast(FP8X4),
+                scales=ws[4 * q : 128, CW * r : CW * r + 512],
+                in_=wg[:],
+            )
+
+        rcs = {}
+
+        def rope_w_unit(q):
+            if q == 0:
+                rcs[0] = (st([P, G1 * 128], U32, "rc", RC0), st([P, 512], U8, "rs", RS0))
+            rc, rs = rcs[0]
+            wr = ring("wr", [P, 4, 4, 128], BF16, WR0, 4096, 3)
+            for l in range(4):
+                g = 4 * q + l
+                nc.sync.dma_start(
+                    out=wr[:, l, :, :],
+                    in_=Wkv_a[512 * g : 512 * (g + 1), 2048:2176].rearrange("(p t) c -> p t c", t=4),
+                )
+            wg = ring("wg", [P, 2048], BF16, WG0, 4096, 2)
+            nc.vector.tensor_copy(
+                out=wg[:].rearrange("p (l c t) -> p l c t", l=4, t=4),
+                in_=wr[:].rearrange("p l t c -> p l c t"),
+            )
+            nc.vector.quantize_mx(
+                out=rc[:, 512 * q : 512 * (q + 1)].bitcast(FP8X4),
+                scales=rs[4 * q : 128, :],
+                in_=wg[:],
+            )
+
+        def cell(out_ap, i, wc, ws, width):
+            for g in range(G1):
+                q, r = divmod(g, 4)
+                nc.tensor.matmul_mx(
+                    out=out_ap,
+                    lhsT=xc[i][:, 128 * g : 128 * (g + 1)].bitcast(FP8X4),
+                    lhsT_scale=xs[i][4 * q : 128, 128 * r : 128 * (r + 1)],
+                    rhs=wc[:, width * g : width * (g + 1)].bitcast(FP8X4),
+                    rhs_scale=ws[4 * q : 128, width * r : width * (r + 1)],
+                    start=(g == 0),
+                    stop=(g == G1 - 1),
+                )
+
+        def pair_cells(i, j, two_banks=False):
+            wc, ws = wch[j]
+            bk = bank()
+            halves = [bk[:, 0:CW], bk[:, CW : 2 * CW]]
+            if two_banks:
+                bk2 = bank()
+                halves[1] = bk2[:, 0:CW]
+            cell(halves[0], i, wc, ws, CW)
+            cell(halves[1], i + 1, wc, ws, CW)
+            return halves
+
+        def square(src_ap, i, j):
+            nc.scalar.activation(
+                out=junk[:], in_=src_ap, func=ACT.Square, accum_out=ssq[:, NCH * i + j : NCH * i + j + 1]
+            )
+
+        def evac_store(halves, i, j):
+            cs = ring("cs", [P, 512], F32, CS0, 2048, 3)
+            for e in range(2):
+                nc.scalar.copy(out=cs[:, CW * e : CW * (e + 1)], in_=halves[e])
+            for e in range(2):
+                square(cs[:, CW * e : CW * (e + 1)], i + e, j)
+            nc.scalar.dma_start(
+                out=o_k[128 * i : 128 * (i + 2), CW * j : CW * (j + 1)].rearrange("(t p) c -> p t c", p=P),
+                in_=cs[:].rearrange("p (t c) -> p t c", t=2),
+            )
+
+        tabs = {}
+
+        def build_rope_tables():
+            s0 = XR0
+            pos_i = st([P, 8], I32, "pos_i", s0)
+            pos = st([P, 8], F32, "pos", s0 + 64)
+            th = st([P, 8, 64], F32, "th", s0 + 128)
+            tm = st([P, 8, 64], F32, "tm", s0 + 128 + 2048)
+            tl = st([P, 8, 64], F32, "tl", s0 + 128 + 4096)
+            ki = st([P, 512], I32, "ki", s0 + 128 + 6144)
+            kf = st([P, 512], F32, "kf", s0 + 128 + 8192)
+            fr = st([P, 2, 512], F32, "fr", s0 + 128 + 10240)
+            zz = st([P, 1024], F32, "zz", s0 + 128 + 14336)
+            nc.gpsimd.iota(pos_i[:], pattern=[[128, 8]], base=0, channel_multiplier=1)
+            nc.vector.tensor_copy(out=pos[:], in_=pos_i[:])
+            for i in range(64):
+                parts = split3(pow(10000.0, -i / 64.0) / TWO_PI)
+                for dst, c in zip((th, tm, tl), parts):
+                    nc.gpsimd.tensor_scalar(
+                        out=dst[:, :, i], in0=pos[:], scalar1=c, scalar2=0.0, op0=ALU.mult, op1=ALU.add
+                    )
+            thf = th[:].rearrange("p a i -> p (a i)")
+            nc.vector.tensor_copy(out=ki[:], in_=thf)
+            nc.vector.tensor_copy(out=kf[:], in_=ki[:])
+            nc.vector.tensor_tensor(out=fr[:, 0, :], in0=thf, in1=kf[:], op=ALU.subtract)
+            nc.vector.tensor_tensor(out=fr[:, 0, :], in0=fr[:, 0, :], in1=tm[:].rearrange("p a i -> p (a i)"), op=ALU.add)
+            nc.vector.tensor_tensor(out=fr[:, 0, :], in0=fr[:, 0, :], in1=tl[:].rearrange("p a i -> p (a i)"), op=ALU.add)
+            nc.vector.tensor_scalar_add(out=fr[:, 1, :], in0=fr[:, 0, :], scalar1=0.25)
+            frf = fr[:].rearrange("p w n -> p (w n)")
+            nc.vector.scalar_tensor_tensor(out=zz[:], in0=frf, scalar=0.5, in1=frf, op0=ALU.is_gt, op1=ALU.subtract)
+            nc.vector.scalar_tensor_tensor(out=frf, in0=zz[:], scalar=0.5, in1=zz[:], op0=ALU.is_gt, op1=ALU.subtract)
+            cf = st([P, 8, 64, 2], F32, "cf", CF0)
+            sf = st([P, 8, 64, 2], F32, "sf", SF0)
+            sin_in = fr[:, 0, :].rearrange("p (a i) -> p a i", a=8)
+            cos_in = fr[:, 1, :].rearrange("p (a i) -> p a i", a=8)
+            nc.scalar.activation(out=cf[:, :, :, 0], in_=cos_in, func=ACT.Sin, scale=TWO_PI)
+            nc.scalar.activation(out=cf[:, :, :, 1], in_=cos_in, func=ACT.Sin, scale=TWO_PI)
+            nc.scalar.activation(out=sf[:, :, :, 0], in_=sin_in, func=ACT.Sin, scale=-TWO_PI)
+            nc.scalar.activation(out=sf[:, :, :, 1], in_=sin_in, func=ACT.Sin, scale=TWO_PI)
+            tabs["cf"] = cf
+            tabs["sf"] = sf
+
+        wb = {}
+
+        def wb_unit(s, g, copies):
+            if g == 0:
+                base = WBC_OFF[s % 2]
+                wb[s] = []
+                for w in range(2):
+                    wbc_t = st([P, G2 * 512], U32, "wbc%d_%d" % (s % 2, w), base + 8192 * w)
+                    wbs_t = st([P, G2 * 512], U8, "wbs%d_%d" % (s % 2, w), base + 16384 + 2048 * w)
+                    wb[s].append((wbc_t, wbs_t))
+            wbr = ring("wbr", [P, 4, 1024], BF16, WBR0, 8192, 2)
+            nc.sync.dma_start(
+                out=wbr[:],
+                in_=Wkv_b[512 * g : 512 * (g + 1), 1024 * s : 1024 * (s + 1)].rearrange("(p t) c -> p t c", t=4),
+            )
+            src = wbr[:].rearrange("p t (h w d) -> p w h d t", w=2, d=128)
+            for w in range(2):
+                wg = ring("wg", [P, 2048], BF16, WG0, 4096, 2)
+                copies[w](out=wg[:].rearrange("p (h d t) -> p h d t", h=4, t=4), in_=src[:, w])
+                nc.vector.quantize_mx(
+                    out=wb[s][w][0][:, 512 * g : 512 * (g + 1)].bitcast(FP8X4),
+                    scales=wb[s][w][1][:, 512 * g : 512 * (g + 1)],
+                    in_=wg[:],
+                )
+
+        for i in range(NT):
+            xc[i] = st([P, G1 * 128], U32, "xc%d" % i, XC0 + 8192 * i)
+            xs[i] = st([P, 512], U8, "xs%d" % i, XS0 + 512 * i)
+            for q in range(4):
+                x_unit(i, q)
+                if i < 2:
+                    wa_unit(0, 4 * i + q)
+            if i % 2 == 1:
+                evac_store(pair_cells(i - 1, 0, two_banks=(i == 1)), i - 1, 0)
+                wa_unit(1, (i - 1) // 2)
+
+        for j in range(1, NCH - 1):
+            for t in range(8):
+                evac_store(pair_cells(2 * t, j), 2 * t, j)
+                wa_unit(j + 1, t)
+                if j == 1 and t == 0:
+                    nc.sync.dma_start(out=gain[:], in_=kv_norm_w.partition_broadcast(P))
+                    build_rope_tables()
+                if j == 2 and t < 4:
+                    rope_w_unit(t)
+
+        rc, rs = rcs[0]
+        cf = tabs["cf"]
+        sf = tabs["sf"]
+        for gq in range(4):
+            bk = bank()
+            for e in range(4):
+                cell(bk[:, 128 * e : 128 * (e + 1)], 4 * gq + e, rc, rs, 128)
+            a0 = (4 * gq) % 8
+            t1 = ring("cs", [P, 512], F32, CS0, 2048, 3)
+            t2 = ring("cs", [P, 512], F32, CS0, 2048, 3)
+            nc.vector.tensor_tensor(
+                out=t1[:], in0=bk[:], in1=cf[:, a0 : a0 + 4].rearrange("p a i e -> p (a i e)"), op=ALU.mult
+            )
+            bv = bk[:].rearrange("p (n e) -> p n e", e=2)
+            sv = sf[:, a0 : a0 + 4].rearrange("p a i e -> p (a i) e")
+            t2v = t2[:].rearrange("p (n e) -> p n e", e=2)
+            nc.vector.tensor_tensor(out=t2v[:, :, 0], in0=bv[:, :, 1], in1=sv[:, :, 0], op=ALU.mult)
+            nc.vector.tensor_tensor(out=t2v[:, :, 1], in0=bv[:, :, 0], in1=sv[:, :, 1], op=ALU.mult)
+            nc.vector.tensor_tensor(out=t1[:], in0=t1[:], in1=t2[:], op=ALU.add)
+            nc.sync.dma_start(
+                out=o_r[512 * gq : 512 * (gq + 1), :].rearrange("(t p) d -> p t d", p=P),
+                in_=t1[:].rearrange("p (t d) -> p t d", t=4),
+            )
+            wb_unit(0, gq, (nc.vector.tensor_copy, nc.scalar.copy))
+
+        cbs = {}
+        rstd = {}
+        ncod = {}
+        nsc = {}
+
+        def reload(t):
+            for e in range(2):
+                slot = (2 * t + e) % 4
+                cb = st([P, 2048], F32, "cb%d" % slot, CB_OFF[slot])
+                i = 2 * t + e
+                nc.sync.dma_start(out=cb[:, 0 : CW * (NCH - 1)], in_=o_k[128 * i : 128 * (i + 1), 0 : CW * (NCH - 1)])
+                cbs[i] = cb
+
+        def small(tag, t, k):
+            return st([P, 2], F32, "%s%d" % (tag, t % 2), SM0 + 64 * (1 + 2 * k + t % 2))
+
+        def last_chunk(t):
+            halves = pair_cells(2 * t, NCH - 1)
+            for e in range(2):
+                i = 2 * t + e
+                tail = cbs[i][:, CW * (NCH - 1) : CW * NCH]
+                nc.scalar.copy(out=tail, in_=halves[e])
+                square(tail, i, NCH - 1)
+            ss = small("ss", t, 0)
+            ms = small("ms", t, 1)
+            y0 = small("y0", t, 2)
+            aa = small("aa", t, 3)
+            yy = small("yy", t, 4)
+            nc.vector.tensor_reduce(
+                out=ss[:],
+                in_=ssq[:, 2 * NCH * t : 2 * NCH * (t + 1)].rearrange("p (e j) -> p e j", e=2),
+                axis=AX.X,
+                op=ALU.add,
+            )
+            nc.gpsimd.tensor_scalar(out=ms[:], in0=ss[:], scalar1=1.0 / 2048.0, scalar2=EPS, op0=ALU.mult, op1=ALU.add)
+            nc.gpsimd.tensor_tensor(out=y0[:], in0=ms[:], in1=neghalf[:], op=ALU.pow)
+            nc.gpsimd.tensor_tensor(out=aa[:], in0=y0[:], in1=y0[:], op=ALU.mult)
+            nc.gpsimd.tensor_tensor(out=aa[:], in0=aa[:], in1=ms[:], op=ALU.mult)
+            nc.gpsimd.tensor_scalar(out=aa[:], in0=aa[:], scalar1=-0.5, scalar2=1.5, op0=ALU.mult, op1=ALU.add)
+            nc.gpsimd.tensor_tensor(out=yy[:], in0=y0[:], in1=aa[:], op=ALU.mult)
+            rstd[t] = yy
+
+        def n_prep(t):
+            for e in range(2):
+                i = 2 * t + e
+                a, b4 = i % 4, i // 4
+                nb = ring_at("nb", [P, 2048], BF16, NB_OFF)
+                nc.vector.scalar_tensor_tensor(
+                    out=nb[:], in0=cbs[i][:], scalar=rstd[t][:, e : e + 1], in1=gain[:], op0=ALU.mult, op1=ALU.mult
+                )
+                ng = ring_at("ng", [P, 2048], BF16, NG_OFF)
+                turn(nb, ng, nc.scalar.copy)
+                ncod[i] = st([P, G2 * 128], U32, "nc%d" % i, NC0 + 2048 * i)
+                if a == 0:
+                    nsc[b4] = st([P, 512], U8, "ns%d" % b4, XS0 + 512 * b4)
+                nc.vector.quantize_mx(out=ncod[i][:].bitcast(FP8X4), scales=nsc[b4][4 * a : 128, :], in_=ng[:])
+
+        reload(0)
+        for t in range(9):
+            if t < 8:
+                last_chunk(t)
+            if t >= 1:
+                n_prep(t - 1)
+            if t + 1 < 8:
+                reload(t + 1)
+            if t >= 5:
+                wb_unit(1, t - 5, (nc.scalar.copy, nc.scalar.copy))
+
+        for s in range(4):
+            for w in range(2):
+                dst = o_k if w == 0 else o_v
+                wbc, wbs = wb[s][w]
+                for i in range(NT):
+                    a, b4 = i % 4, i // 4
+                    bk = bank()
+                    for g in range(G2):
+                        nc.tensor.matmul_mx(
+                            out=bk[:],
+                            lhsT=ncod[i][:, 128 * g : 128 * (g + 1)].bitcast(FP8X4),
+                            lhsT_scale=nsc[b4][4 * a : 128, 128 * g : 128 * (g + 1)],
+                            rhs=wbc[:, 512 * g : 512 * (g + 1)].bitcast(FP8X4),
+                            rhs_scale=wbs[:, 512 * g : 512 * (g + 1)],
+                            start=(g == 0),
+                            stop=(g == G2 - 1),
+                        )
+                    osb = ring("os", [P, 512], F32, OS0, 2048, 8)
+                    if i % 2 == 0:
+                        nc.scalar.copy(out=osb[:], in_=bk[:])
+                        nc.scalar.dma_start(out=dst[128 * i : 128 * (i + 1), 512 * s : 512 * (s + 1)], in_=osb[:])
+                    else:
+                        nc.vector.tensor_copy(out=osb[:], in_=bk[:])
+                        nc.sync.dma_start(out=dst[128 * i : 128 * (i + 1), 512 * s : 512 * (s + 1)], in_=osb[:])
+                    if 1 <= s <= 2 and w == 0 and i % 4 == 0:
+                        wb_unit(s + 1, i // 4, (nc.vector.tensor_copy, nc.scalar.copy))

@@ -43,13 +43,18 @@ ID0 = GN0 + 4096
 SQ0 = ID0 + 512
 JK0 = SQ0 + 512
 SM0 = JK0 + 512
+XR_OFF = (XR0, XR0 + 4096, XR0 + 8192, RC0, RC0 + 4096, CF0)
+XG_OFF = (XG0, XG0 + 4096, SF0)
 CB_OFF = (WR0, WR0 + 8192, XC0, XC0 + 8192)
 NB_OFF = (WR0 + 16384, WR0 + 20480)
 NG_OFF = (WR0 + 24576, CS0)
 NC0 = XC0 + 2 * 8192
-WBR0 = WC0
+WBR_OFF = (WC0, WC0 + 8192, WC0 + 16384, WC0 + 24576)
 WBC_OFF = (XR0, XC0 + 6 * 8192)
 OS0 = XC0 + 9 * 8192
+
+M_START = 6
+HEAD_UNITS = 8
 
 
 def split3(c):
@@ -71,24 +76,26 @@ def tile_multiheadlatentattention_pa_l_kernel(tc, x, Wkv_a, kv_norm_w, Wkv_b, ou
 
     with ExitStack() as ctx:
         sb = ctx.enter_context(tc.tile_pool(name="sb", bufs=1))
-        ps = ctx.enter_context(tc.psum_pool(name="ps", bufs=8))
-        cnt = {"wr": 0, "wg": 0, "xr": 0, "xg": 0, "cs": 0, "wbr": 0, "nb": 0, "ng": 0, "os": 0}
+        ps = ctx.enter_context(tc.psum_pool(name="ps", bufs=1))
+        ctx.enter_context(tc.manual_schedule())
+        cnt = {}
 
         def st(shape, dtype, tag, offset):
             return sb.tile(shape, dtype, name=tag, tag=tag, offset=offset, align_bytes=64)
 
-        def ring(kind, shape, dtype, base, size, depth):
-            n = cnt[kind] % depth
-            cnt[kind] = cnt[kind] + 1
-            return st(shape, dtype, "%s%d" % (kind, n), base + size * n)
-
         def ring_at(kind, shape, dtype, offsets):
-            n = cnt[kind] % len(offsets)
-            cnt[kind] = cnt[kind] + 1
+            n = cnt.get(kind, 0) % len(offsets)
+            cnt[kind] = cnt.get(kind, 0) + 1
             return st(shape, dtype, "%s%d" % (kind, n), offsets[n])
 
-        def bank():
-            return ps.tile([P, 512], F32, name="bank", tag="bank")
+        def ring(kind, shape, dtype, base, size, depth):
+            return ring_at(kind, shape, dtype, [base + size * n for n in range(depth)])
+
+        def tp_bank():
+            return ps.tile([P, 512], F32, name="tp", tag="tp", bufs=5)
+
+        def acc_bank():
+            return ps.tile([P, 512], F32, name="acc", tag="acc", bufs=3)
 
         ident = st([P, P], F32, "ident", ID0)
         masks.make_identity(nc, ident[:])
@@ -102,11 +109,11 @@ def tile_multiheadlatentattention_pa_l_kernel(tc, x, Wkv_a, kv_norm_w, Wkv_b, ou
         xs = {}
         wch = {}
 
-        def turn(src, dst, copy):
+        def turn_pe(src):
             words = src[:].bitcast(F32)
-            dstw = dst[:].bitcast(F32)
+            banks = []
             for hb in range(2):
-                bk = bank()
+                bk = tp_bank()
                 for l in range(2):
                     for u in range(2):
                         lo = 256 * (2 * hb + l)
@@ -115,74 +122,85 @@ def tile_multiheadlatentattention_pa_l_kernel(tc, x, Wkv_a, kv_norm_w, Wkv_b, ou
                             words[:, lo + u : lo + 256 : 2],
                             ident[:],
                         )
-                copy(
-                    out=dstw[:, 512 * hb : 512 * (hb + 1)].rearrange("p (l m u) -> p l m u", l=2, u=2),
-                    in_=bk[:].rearrange("p (l u m) -> p l m u", l=2, u=2),
-                )
+                banks.append(bk)
+            return banks
 
-        def x_unit(i, q):
-            xr = ring("xr", [P, 2048], BF16, XR0, 4096, 3)
-            nc.sync.dma_start(out=xr[:], in_=xf[128 * i : 128 * (i + 1), 2048 * q : 2048 * (q + 1)])
-            xg = ring("xg", [P, 2048], BF16, XG0, 4096, 2)
-            turn(xr, xg, nc.scalar.copy)
+        def turn_copy(banks, dst, hb, copy):
+            copy(
+                out=dst[:].bitcast(F32)[:, 512 * hb : 512 * (hb + 1)].rearrange("p (l m u) -> p l m u", l=2, u=2),
+                in_=banks[hb][:].rearrange("p (l u m) -> p l m u", l=2, u=2),
+            )
+
+        xr = {}
+        xb = {}
+        xg = {}
+
+        def x_load(n):
+            i, q = divmod(n, 4)
+            xr[n] = ring_at("xr", [P, 2048], BF16, XR_OFF)
+            nc.sync.dma_start(out=xr[n][:], in_=xf[128 * i : 128 * (i + 1), 2048 * q : 2048 * (q + 1)])
+
+        def x_turn(n):
+            xb[n] = turn_pe(xr[n])
+
+        def x_quant(n):
+            i, q = divmod(n, 4)
+            if q == 0:
+                xc[i] = st([P, G1 * 128], U32, "xc%d" % i, XC0 + 8192 * i)
+                xs[i] = st([P, 512], U8, "xs%d" % i, XS0 + 512 * i)
             nc.vector.quantize_mx(
                 out=xc[i][:, 512 * q : 512 * (q + 1)].bitcast(FP8X4),
                 scales=xs[i][4 * q : 128, :],
-                in_=xg[:],
+                in_=xg[n][:],
             )
 
-        def wa_unit(j, s):
+        wraw = {}
+        wgrp = {}
+
+        def wa_load(j, s):
+            wraw[s] = ring("wr", [P, 2, 4, CW], BF16, WR0, 4096, 3)
+            for l in range(2):
+                g = 2 * s + l
+                nc.sync.dma_start(
+                    out=wraw[s][:, l, :, :],
+                    in_=Wkv_a[512 * g : 512 * (g + 1), CW * j : CW * (j + 1)].rearrange("(p t) c -> p t c", t=4),
+                )
+
+        def wa_copy(j, s):
+            wgrp[s] = ring("wg", [P, 2048], BF16, WG0, 4096, 2)
+            nc.vector.tensor_copy(
+                out=wgrp[s][:].rearrange("p (l c t) -> p l c t", l=2, t=4),
+                in_=wraw[s][:].rearrange("p l t c -> p l c t"),
+            )
+
+        def wa_quant(j, s):
             if s == 0:
                 wch[j] = (
                     st([P, G1 * CW], U32, "wc%d" % (j % 2), WC0 + 16384 * (j % 2)),
                     st([P, 4 * CW], U8, "ws%d" % (j % 2), WS0 + 1024 * (j % 2)),
                 )
             wc, ws = wch[j]
-            wr = ring("wr", [P, 2, 4, CW], BF16, WR0, 4096, 3)
-            for l in range(2):
-                g = 2 * s + l
-                nc.sync.dma_start(
-                    out=wr[:, l, :, :],
-                    in_=Wkv_a[512 * g : 512 * (g + 1), CW * j : CW * (j + 1)].rearrange("(p t) c -> p t c", t=4),
-                )
-            wg = ring("wg", [P, 2048], BF16, WG0, 4096, 2)
-            nc.vector.tensor_copy(
-                out=wg[:].rearrange("p (l c t) -> p l c t", l=2, t=4),
-                in_=wr[:].rearrange("p l t c -> p l c t"),
-            )
             q, r = divmod(2 * s, 4)
             nc.vector.quantize_mx(
                 out=wc[:, 512 * s : 512 * (s + 1)].bitcast(FP8X4),
                 scales=ws[4 * q : 128, CW * r : CW * r + 512],
-                in_=wg[:],
+                in_=wgrp[s][:],
             )
 
-        rcs = {}
+        def wa_tick(j, s):
+            if s == -1:
+                wa_load(j, 0)
+                wa_load(j, 1)
+                return
+            if s + 2 < 8:
+                wa_load(j, s + 2)
+            if s < 8:
+                wa_copy(j, s)
+            if s >= 1:
+                wa_quant(j, s - 1)
 
-        def rope_w_unit(q):
-            if q == 0:
-                rcs[0] = (st([P, G1 * 128], U32, "rc", RC0), st([P, 512], U8, "rs", RS0))
-            rc, rs = rcs[0]
-            wr = ring("wr", [P, 4, 4, 128], BF16, WR0, 4096, 3)
-            for l in range(4):
-                g = 4 * q + l
-                nc.sync.dma_start(
-                    out=wr[:, l, :, :],
-                    in_=Wkv_a[512 * g : 512 * (g + 1), 2048:2176].rearrange("(p t) c -> p t c", t=4),
-                )
-            wg = ring("wg", [P, 2048], BF16, WG0, 4096, 2)
-            nc.vector.tensor_copy(
-                out=wg[:].rearrange("p (l c t) -> p l c t", l=4, t=4),
-                in_=wr[:].rearrange("p l t c -> p l c t"),
-            )
-            nc.vector.quantize_mx(
-                out=rc[:, 512 * q : 512 * (q + 1)].bitcast(FP8X4),
-                scales=rs[4 * q : 128, :],
-                in_=wg[:],
-            )
-
-        def cell(out_ap, i, wc, ws, width):
-            for g in range(G1):
+        def cell_part(out_ap, i, wc, ws, width, g0, g1):
+            for g in range(g0, g1):
                 q, r = divmod(g, 4)
                 nc.tensor.matmul_mx(
                     out=out_ap,
@@ -194,26 +212,21 @@ def tile_multiheadlatentattention_pa_l_kernel(tc, x, Wkv_a, kv_norm_w, Wkv_b, ou
                     stop=(g == G1 - 1),
                 )
 
-        def pair_cells(i, j, two_banks=False):
+        def pair_cells(i, j):
             wc, ws = wch[j]
-            bk = bank()
-            halves = [bk[:, 0:CW], bk[:, CW : 2 * CW]]
-            if two_banks:
-                bk2 = bank()
-                halves[1] = bk2[:, 0:CW]
-            cell(halves[0], i, wc, ws, CW)
-            cell(halves[1], i + 1, wc, ws, CW)
-            return halves
+            bk = acc_bank()
+            cell_part(bk[:, 0:CW], i, wc, ws, CW, 0, G1)
+            cell_part(bk[:, CW : 2 * CW], i + 1, wc, ws, CW, 0, G1)
+            return bk
 
         def square(src_ap, i, j):
             nc.scalar.activation(
                 out=junk[:], in_=src_ap, func=ACT.Square, accum_out=ssq[:, NCH * i + j : NCH * i + j + 1]
             )
 
-        def evac_store(halves, i, j):
+        def evac_store(bk, i, j):
             cs = ring("cs", [P, 512], F32, CS0, 2048, 3)
-            for e in range(2):
-                nc.scalar.copy(out=cs[:, CW * e : CW * (e + 1)], in_=halves[e])
+            nc.scalar.copy(out=cs[:], in_=bk[:])
             for e in range(2):
                 square(cs[:, CW * e : CW * (e + 1)], i + e, j)
             nc.scalar.dma_start(
@@ -223,31 +236,36 @@ def tile_multiheadlatentattention_pa_l_kernel(tc, x, Wkv_a, kv_norm_w, Wkv_b, ou
 
         tabs = {}
 
-        def build_rope_tables():
+        def rope_tables_pool():
             s0 = XR0
             pos_i = st([P, 8], I32, "pos_i", s0)
             pos = st([P, 8], F32, "pos", s0 + 64)
-            th = st([P, 8, 64], F32, "th", s0 + 128)
-            tm = st([P, 8, 64], F32, "tm", s0 + 128 + 2048)
-            tl = st([P, 8, 64], F32, "tl", s0 + 128 + 4096)
-            ki = st([P, 512], I32, "ki", s0 + 128 + 6144)
-            kf = st([P, 512], F32, "kf", s0 + 128 + 8192)
-            fr = st([P, 2, 512], F32, "fr", s0 + 128 + 10240)
-            zz = st([P, 1024], F32, "zz", s0 + 128 + 14336)
+            tabs["th"] = st([P, 8, 64], F32, "th", s0 + 128)
+            tabs["tm"] = st([P, 8, 64], F32, "tm", s0 + 128 + 2048)
+            tabs["tl"] = st([P, 8, 64], F32, "tl", s0 + 128 + 4096)
             nc.gpsimd.iota(pos_i[:], pattern=[[128, 8]], base=0, channel_multiplier=1)
             nc.vector.tensor_copy(out=pos[:], in_=pos_i[:])
             for i in range(64):
                 parts = split3(pow(10000.0, -i / 64.0) / TWO_PI)
-                for dst, c in zip((th, tm, tl), parts):
+                for key, c in zip(("th", "tm", "tl"), parts):
                     nc.gpsimd.tensor_scalar(
-                        out=dst[:, :, i], in0=pos[:], scalar1=c, scalar2=0.0, op0=ALU.mult, op1=ALU.add
+                        out=tabs[key][:, :, i], in0=pos[:], scalar1=c, scalar2=0.0, op0=ALU.mult, op1=ALU.add
                     )
-            thf = th[:].rearrange("p a i -> p (a i)")
+
+        def rope_tables_finish():
+            s0 = XR0
+            ki = st([P, 512], I32, "ki", s0 + 128 + 6144)
+            kf = st([P, 512], F32, "kf", s0 + 128 + 8192)
+            fr = st([P, 2, 512], F32, "fr", s0 + 128 + 10240)
+            zz = st([P, 1024], F32, "zz", s0 + 128 + 14336)
+            thf = tabs["th"][:].rearrange("p a i -> p (a i)")
             nc.vector.tensor_copy(out=ki[:], in_=thf)
             nc.vector.tensor_copy(out=kf[:], in_=ki[:])
             nc.vector.tensor_tensor(out=fr[:, 0, :], in0=thf, in1=kf[:], op=ALU.subtract)
-            nc.vector.tensor_tensor(out=fr[:, 0, :], in0=fr[:, 0, :], in1=tm[:].rearrange("p a i -> p (a i)"), op=ALU.add)
-            nc.vector.tensor_tensor(out=fr[:, 0, :], in0=fr[:, 0, :], in1=tl[:].rearrange("p a i -> p (a i)"), op=ALU.add)
+            for key in ("tm", "tl"):
+                nc.vector.tensor_tensor(
+                    out=fr[:, 0, :], in0=fr[:, 0, :], in1=tabs[key][:].rearrange("p a i -> p (a i)"), op=ALU.add
+                )
             nc.vector.tensor_scalar_add(out=fr[:, 1, :], in0=fr[:, 0, :], scalar1=0.25)
             frf = fr[:].rearrange("p w n -> p (w n)")
             nc.vector.scalar_tensor_tensor(out=zz[:], in0=frf, scalar=0.5, in1=frf, op0=ALU.is_gt, op1=ALU.subtract)
@@ -263,59 +281,151 @@ def tile_multiheadlatentattention_pa_l_kernel(tc, x, Wkv_a, kv_norm_w, Wkv_b, ou
             tabs["cf"] = cf
             tabs["sf"] = sf
 
-        wb = {}
+        rraw = {}
+        rgrp = {}
 
-        def wb_unit(s, g, copies):
-            if g == 0:
-                base = WBC_OFF[s % 2]
-                wb[s] = []
-                for w in range(2):
-                    wbc_t = st([P, G2 * 512], U32, "wbc%d_%d" % (s % 2, w), base + 8192 * w)
-                    wbs_t = st([P, G2 * 512], U8, "wbs%d_%d" % (s % 2, w), base + 16384 + 2048 * w)
-                    wb[s].append((wbc_t, wbs_t))
-            wbr = ring("wbr", [P, 4, 1024], BF16, WBR0, 8192, 2)
-            nc.sync.dma_start(
-                out=wbr[:],
-                in_=Wkv_b[512 * g : 512 * (g + 1), 1024 * s : 1024 * (s + 1)].rearrange("(p t) c -> p t c", t=4),
-            )
-            src = wbr[:].rearrange("p t (h w d) -> p w h d t", w=2, d=128)
-            for w in range(2):
-                wg = ring("wg", [P, 2048], BF16, WG0, 4096, 2)
-                copies[w](out=wg[:].rearrange("p (h d t) -> p h d t", h=4, t=4), in_=src[:, w])
-                nc.vector.quantize_mx(
-                    out=wb[s][w][0][:, 512 * g : 512 * (g + 1)].bitcast(FP8X4),
-                    scales=wb[s][w][1][:, 512 * g : 512 * (g + 1)],
-                    in_=wg[:],
+        def rope_w_load(q):
+            rraw[q] = st([P, 4, 4, 128], BF16, "rr%d" % q, XR0 + 4096 * q)
+            for l in range(4):
+                g = 4 * q + l
+                nc.sync.dma_start(
+                    out=rraw[q][:, l, :, :],
+                    in_=Wkv_a[512 * g : 512 * (g + 1), 2048:2176].rearrange("(p t) c -> p t c", t=4),
                 )
 
-        for i in range(NT):
-            xc[i] = st([P, G1 * 128], U32, "xc%d" % i, XC0 + 8192 * i)
-            xs[i] = st([P, 512], U8, "xs%d" % i, XS0 + 512 * i)
-            for q in range(4):
-                x_unit(i, q)
-                if i < 2:
-                    wa_unit(0, 4 * i + q)
-            if i % 2 == 1:
-                evac_store(pair_cells(i - 1, 0, two_banks=(i == 1)), i - 1, 0)
-                wa_unit(1, (i - 1) // 2)
+        def rope_w_copy(q):
+            rgrp[q] = st([P, 2048], BF16, "rg", XG0 + 4096)
+            nc.vector.tensor_copy(
+                out=rgrp[q][:].rearrange("p (l c t) -> p l c t", l=4, t=4),
+                in_=rraw[q][:].rearrange("p l t c -> p l c t"),
+            )
+
+        def rope_w_quant(q):
+            if q == 0:
+                tabs["rc"] = st([P, G1 * 128], U32, "rc", RC0)
+                tabs["rs"] = st([P, 512], U8, "rs", RS0)
+            nc.vector.quantize_mx(
+                out=tabs["rc"][:, 512 * q : 512 * (q + 1)].bitcast(FP8X4),
+                scales=tabs["rs"][4 * q : 128, :],
+                in_=rgrp[q][:],
+            )
+
+        wb = {}
+        wbraw = {}
+        wbgrp = {}
+
+        def wb_load(s, g, depth):
+            wbraw[g] = ring_at("wbr", [P, 4, 1024], BF16, WBR_OFF[0:depth])
+            nc.sync.dma_start(
+                out=wbraw[g][:],
+                in_=Wkv_b[512 * g : 512 * (g + 1), 1024 * s : 1024 * (s + 1)].rearrange("(p t) c -> p t c", t=4),
+            )
+
+        def wb_copy(s, g, w, copy):
+            wbgrp[w] = ring("wg", [P, 2048], BF16, WG0, 4096, 2)
+            src = wbraw[g][:].rearrange("p t (h w d) -> p w h d t", w=2, d=128)
+            copy(out=wbgrp[w][:].rearrange("p (h d t) -> p h d t", h=4, t=4), in_=src[:, w])
+
+        def wb_quant(s, g, w):
+            if g == 0 and w == 0:
+                base = WBC_OFF[s % 2]
+                wb[s] = []
+                for v in range(2):
+                    wbc_t = st([P, G2 * 512], U32, "wbc%d_%d" % (s % 2, v), base + 8192 * v)
+                    wbs_t = st([P, G2 * 512], U8, "wbs%d_%d" % (s % 2, v), base + 16384 + 2048 * v)
+                    wb[s].append((wbc_t, wbs_t))
+            nc.vector.quantize_mx(
+                out=wb[s][w][0][:, 512 * g : 512 * (g + 1)].bitcast(FP8X4),
+                scales=wb[s][w][1][:, 512 * g : 512 * (g + 1)],
+                in_=wbgrp[w][:],
+            )
+
+        state = {"next_half": 0}
+        acc0 = {}
+
+        def m_half(k):
+            i, part = divmod(k, 2)
+            if i % 2 == 0 and part == 0:
+                acc0[i // 2] = acc_bank()
+            bk = acc0[i // 2]
+            wc, ws = wch[0]
+            cell_part(bk[:, CW * (i % 2) : CW * (i % 2 + 1)], i, wc, ws, CW, 8 * part, 8 * part + 8)
+            if i % 2 == 1 and part == 1:
+                evac_store(bk, i - 1, 0)
+
+        x_load(0)
+        x_load(1)
+        wa_tick(0, -1)
+        x_load(2)
+        x_load(3)
+        for h in range(2 * NT):
+            n0 = 2 * h
+            for n in (n0 + 4, n0 + 5):
+                if n < 4 * NT:
+                    x_load(n)
+            x_turn(n0)
+            x_turn(n0 + 1)
+            for n in (n0, n0 + 1):
+                xg[n] = ring_at("xg", [P, 2048], BF16, XG_OFF)
+            turn_copy(xb[n0], xg[n0], 0, nc.scalar.copy)
+            turn_copy(xb[n0], xg[n0], 1, nc.scalar.copy)
+            turn_copy(xb[n0 + 1], xg[n0 + 1], 0, nc.scalar.copy)
+            if n0 < HEAD_UNITS:
+                turn_copy(xb[n0 + 1], xg[n0 + 1], 1, nc.scalar.copy)
+                wa_tick(0, n0)
+                x_quant(n0)
+                wa_tick(0, n0 + 1)
+                x_quant(n0 + 1)
+            else:
+                x_quant(n0)
+                turn_copy(xb[n0 + 1], xg[n0 + 1], 1, nc.vector.tensor_copy)
+                if n0 == HEAD_UNITS:
+                    wa_tick(0, 8)
+                if h >= 7 and h % 2 == 1 and (h - 9) // 2 <= 8:
+                    wa_tick(1, (h - 9) // 2)
+                x_quant(n0 + 1)
+            issued = 0
+            while h >= M_START and state["next_half"] <= h - 2 and issued < 2:
+                m_half(state["next_half"])
+                state["next_half"] = state["next_half"] + 1
+                issued = issued + 1
+        while state["next_half"] < 2 * NT:
+            m_half(state["next_half"])
+            state["next_half"] = state["next_half"] + 1
 
         for j in range(1, NCH - 1):
             for t in range(8):
+                if t == 0:
+                    wa_tick(j + 1, -1)
                 evac_store(pair_cells(2 * t, j), 2 * t, j)
-                wa_unit(j + 1, t)
+                if j == 4 and 1 <= t <= 4:
+                    rope_w_copy(t - 1)
+                wa_tick(j + 1, t)
+                if t == 7:
+                    wa_tick(j + 1, 8)
                 if j == 1 and t == 0:
                     nc.sync.dma_start(out=gain[:], in_=kv_norm_w.partition_broadcast(P))
-                    build_rope_tables()
-                if j == 2 and t < 4:
-                    rope_w_unit(t)
+                    rope_tables_pool()
+                if j == 3 and t == 0:
+                    rope_tables_finish()
+                if j == 4 and t == 0:
+                    for q in range(4):
+                        rope_w_load(q)
+                if j == 4 and 1 <= t <= 4:
+                    rope_w_quant(t - 1)
 
-        rc, rs = rcs[0]
+        rc = tabs["rc"]
+        rs = tabs["rs"]
         cf = tabs["cf"]
         sf = tabs["sf"]
+        wb_load(0, 0, 2)
+        wb_load(0, 1, 2)
         for gq in range(4):
-            bk = bank()
+            bk = acc_bank()
             for e in range(4):
-                cell(bk[:, 128 * e : 128 * (e + 1)], 4 * gq + e, rc, rs, 128)
+                cell_part(bk[:, 128 * e : 128 * (e + 1)], 4 * gq + e, rc, rs, 128, 0, G1)
+            wb_copy(0, gq, 0, nc.vector.tensor_copy)
+            wb_copy(0, gq, 1, nc.scalar.copy)
             a0 = (4 * gq) % 8
             t1 = ring("cs", [P, 512], F32, CS0, 2048, 3)
             t2 = ring("cs", [P, 512], F32, CS0, 2048, 3)
@@ -332,31 +442,36 @@ def tile_multiheadlatentattention_pa_l_kernel(tc, x, Wkv_a, kv_norm_w, Wkv_b, ou
                 out=o_r[512 * gq : 512 * (gq + 1), :].rearrange("(t p) d -> p t d", p=P),
                 in_=t1[:].rearrange("p (t d) -> p t d", t=4),
             )
-            wb_unit(0, gq, (nc.vector.tensor_copy, nc.scalar.copy))
+            wb_quant(0, gq, 0)
+            wb_quant(0, gq, 1)
+            if gq + 2 < 4:
+                wb_load(0, gq + 2, 2)
 
         cbs = {}
         rstd = {}
+        nbt = {}
+        nbk = {}
+        ngt = {}
         ncod = {}
         nsc = {}
+        LAST = NCH - 1
 
         def reload(t):
             for e in range(2):
-                slot = (2 * t + e) % 4
-                cb = st([P, 2048], F32, "cb%d" % slot, CB_OFF[slot])
                 i = 2 * t + e
-                nc.sync.dma_start(out=cb[:, 0 : CW * (NCH - 1)], in_=o_k[128 * i : 128 * (i + 1), 0 : CW * (NCH - 1)])
-                cbs[i] = cb
+                cbs[i] = st([P, 2048], F32, "cb%d" % (i % 4), CB_OFF[i % 4])
+                nc.sync.dma_start(out=cbs[i][:, 0 : CW * LAST], in_=o_k[128 * i : 128 * (i + 1), 0 : CW * LAST])
 
         def small(tag, t, k):
             return st([P, 2], F32, "%s%d" % (tag, t % 2), SM0 + 64 * (1 + 2 * k + t % 2))
 
-        def last_chunk(t):
-            halves = pair_cells(2 * t, NCH - 1)
+        def last_evac(t, bk):
             for e in range(2):
-                i = 2 * t + e
-                tail = cbs[i][:, CW * (NCH - 1) : CW * NCH]
-                nc.scalar.copy(out=tail, in_=halves[e])
-                square(tail, i, NCH - 1)
+                nc.scalar.copy(out=cbs[2 * t + e][:, CW * LAST : CW * NCH], in_=bk[:, CW * e : CW * (e + 1)])
+            for e in range(2):
+                square(cbs[2 * t + e][:, CW * LAST : CW * NCH], 2 * t + e, LAST)
+
+        def rstd_chain(t):
             ss = small("ss", t, 0)
             ms = small("ms", t, 1)
             y0 = small("y0", t, 2)
@@ -376,55 +491,91 @@ def tile_multiheadlatentattention_pa_l_kernel(tc, x, Wkv_a, kv_norm_w, Wkv_b, ou
             nc.gpsimd.tensor_tensor(out=yy[:], in0=y0[:], in1=aa[:], op=ALU.mult)
             rstd[t] = yy
 
-        def n_prep(t):
-            for e in range(2):
-                i = 2 * t + e
-                a, b4 = i % 4, i // 4
-                nb = ring_at("nb", [P, 2048], BF16, NB_OFF)
-                nc.vector.scalar_tensor_tensor(
-                    out=nb[:], in0=cbs[i][:], scalar=rstd[t][:, e : e + 1], in1=gain[:], op0=ALU.mult, op1=ALU.mult
-                )
-                ng = ring_at("ng", [P, 2048], BF16, NG_OFF)
-                turn(nb, ng, nc.scalar.copy)
-                ncod[i] = st([P, G2 * 128], U32, "nc%d" % i, NC0 + 2048 * i)
-                if a == 0:
-                    nsc[b4] = st([P, 512], U8, "ns%d" % b4, XS0 + 512 * b4)
-                nc.vector.quantize_mx(out=ncod[i][:].bitcast(FP8X4), scales=nsc[b4][4 * a : 128, :], in_=ng[:])
+        def scale(i):
+            nbt[i] = ring_at("nb", [P, 2048], BF16, NB_OFF)
+            nc.vector.scalar_tensor_tensor(
+                out=nbt[i][:], in0=cbs[i][:], scalar=rstd[i // 2][:, i % 2 : i % 2 + 1], in1=gain[:],
+                op0=ALU.mult, op1=ALU.mult,
+            )
+
+        def n_copy(i):
+            ngt[i] = ring_at("ng", [P, 2048], BF16, NG_OFF)
+            turn_copy(nbk[i], ngt[i], 0, nc.scalar.copy)
+            turn_copy(nbk[i], ngt[i], 1, nc.scalar.copy)
+
+        def n_quant(i):
+            a, b4 = i % 4, i // 4
+            ncod[i] = st([P, G2 * 128], U32, "nc%d" % i, NC0 + 2048 * i)
+            if a == 0:
+                nsc[b4] = st([P, 512], U8, "ns%d" % b4, XS0 + 512 * b4)
+            nc.vector.quantize_mx(out=ncod[i][:].bitcast(FP8X4), scales=nsc[b4][4 * a : 128, :], in_=ngt[i][:])
 
         reload(0)
         for t in range(9):
-            if t < 8:
-                last_chunk(t)
-            if t >= 1:
-                n_prep(t - 1)
-            if t + 1 < 8:
-                reload(t + 1)
-            if t >= 5:
-                wb_unit(1, t - 5, (nc.scalar.copy, nc.scalar.copy))
+            now = t < 8
+            prev = t >= 1
+            if now:
+                bk = pair_cells(2 * t, LAST)
+            if t == 0:
+                reload(1)
+            if prev:
+                nbk[2 * t - 2] = turn_pe(nbt[2 * t - 2])
+                nbk[2 * t - 1] = turn_pe(nbt[2 * t - 1])
+            if now:
+                last_evac(t, bk)
+            if prev:
+                n_copy(2 * t - 2)
+                n_copy(2 * t - 1)
+            if now:
+                rstd_chain(t)
+            if prev:
+                n_quant(2 * t - 2)
+            if now:
+                scale(2 * t)
+            if prev:
+                n_quant(2 * t - 1)
+            if now:
+                scale(2 * t + 1)
+            if t + 2 < 8:
+                reload(t + 2)
 
+        wb_load(1, 0, 4)
+        wb_load(1, 1, 4)
         for s in range(4):
-            for w in range(2):
+            for c in range(2 * NT):
+                w, i = divmod(c, NT)
                 dst = o_k if w == 0 else o_v
                 wbc, wbs = wb[s][w]
-                for i in range(NT):
-                    a, b4 = i % 4, i // 4
-                    bk = bank()
-                    for g in range(G2):
-                        nc.tensor.matmul_mx(
-                            out=bk[:],
-                            lhsT=ncod[i][:, 128 * g : 128 * (g + 1)].bitcast(FP8X4),
-                            lhsT_scale=nsc[b4][4 * a : 128, 128 * g : 128 * (g + 1)],
-                            rhs=wbc[:, 512 * g : 512 * (g + 1)].bitcast(FP8X4),
-                            rhs_scale=wbs[:, 512 * g : 512 * (g + 1)],
-                            start=(g == 0),
-                            stop=(g == G2 - 1),
-                        )
-                    osb = ring("os", [P, 512], F32, OS0, 2048, 8)
-                    if i % 2 == 0:
-                        nc.scalar.copy(out=osb[:], in_=bk[:])
-                        nc.scalar.dma_start(out=dst[128 * i : 128 * (i + 1), 512 * s : 512 * (s + 1)], in_=osb[:])
-                    else:
-                        nc.vector.tensor_copy(out=osb[:], in_=bk[:])
-                        nc.sync.dma_start(out=dst[128 * i : 128 * (i + 1), 512 * s : 512 * (s + 1)], in_=osb[:])
-                    if 1 <= s <= 2 and w == 0 and i % 4 == 0:
-                        wb_unit(s + 1, i // 4, (nc.vector.tensor_copy, nc.scalar.copy))
+                a, b4 = i % 4, i // 4
+                bk = acc_bank() if c % 8 in (0, 3, 6) else tp_bank()
+                for g in range(G2):
+                    nc.tensor.matmul_mx(
+                        out=bk[:],
+                        lhsT=ncod[i][:, 128 * g : 128 * (g + 1)].bitcast(FP8X4),
+                        lhsT_scale=nsc[b4][4 * a : 128, 128 * g : 128 * (g + 1)],
+                        rhs=wbc[:, 512 * g : 512 * (g + 1)].bitcast(FP8X4),
+                        rhs_scale=wbs[:, 512 * g : 512 * (g + 1)],
+                        start=(g == 0),
+                        stop=(g == G2 - 1),
+                    )
+                osb = ring("os", [P, 512], F32, OS0, 2048, 8)
+                if c % 2 == 0:
+                    nc.scalar.copy(out=osb[:], in_=bk[:])
+                    nc.scalar.dma_start(out=dst[128 * i : 128 * (i + 1), 512 * s : 512 * (s + 1)], in_=osb[:])
+                else:
+                    nc.vector.tensor_copy(out=osb[:], in_=bk[:])
+                    nc.sync.dma_start(out=dst[128 * i : 128 * (i + 1), 512 * s : 512 * (s + 1)], in_=osb[:])
+                if s < 3:
+                    g, r = divmod(c, 8)
+                    if r == 0:
+                        wb_copy(s + 1, g, 0, nc.vector.tensor_copy)
+                        wb_copy(s + 1, g, 1, nc.scalar.copy)
+                    if r == 2:
+                        wb_quant(s + 1, g, 0)
+                    if r == 3:
+                        wb_quant(s + 1, g, 1)
+                    if r == 4:
+                        if g + 2 < 4:
+                            wb_load(s + 1, g + 2, 4)
+                        elif s + 2 < 4:
+                            wb_load(s + 2, g - 2, 4)

@@ -53,7 +53,9 @@ WBR_OFF = (WC0, WC0 + 8192, WC0 + 16384, WC0 + 24576)
 WBC_OFF = (XR0, XC0 + 6 * 8192)
 OS0 = XC0 + 9 * 8192
 
-M_START = 6
+M_START = 12
+M_LAG = 6
+N_LAG = 3
 HEAD_UNITS = 8
 
 
@@ -340,17 +342,17 @@ def tile_multiheadlatentattention_pa_l_kernel(tc, x, Wkv_a, kv_norm_w, Wkv_b, ou
                 in_=wbgrp[w][:],
             )
 
-        state = {"next_half": 0}
+        state = {"next_part": 0}
         acc0 = {}
 
-        def m_half(k):
-            i, part = divmod(k, 2)
+        def m_part(k):
+            i, part = divmod(k, 4)
             if i % 2 == 0 and part == 0:
                 acc0[i // 2] = acc_bank()
             bk = acc0[i // 2]
             wc, ws = wch[0]
-            cell_part(bk[:, CW * (i % 2) : CW * (i % 2 + 1)], i, wc, ws, CW, 8 * part, 8 * part + 8)
-            if i % 2 == 1 and part == 1:
+            cell_part(bk[:, CW * (i % 2) : CW * (i % 2 + 1)], i, wc, ws, CW, 4 * part, 4 * part + 4)
+            if i % 2 == 1 and part == 3:
                 evac_store(bk, i - 1, 0)
 
         x_load(0)
@@ -358,40 +360,31 @@ def tile_multiheadlatentattention_pa_l_kernel(tc, x, Wkv_a, kv_norm_w, Wkv_b, ou
         wa_tick(0, -1)
         x_load(2)
         x_load(3)
-        for h in range(2 * NT):
-            n0 = 2 * h
-            for n in (n0 + 4, n0 + 5):
-                if n < 4 * NT:
-                    x_load(n)
-            x_turn(n0)
-            x_turn(n0 + 1)
-            for n in (n0, n0 + 1):
+        for n in range(4 * NT + 1):
+            if n + 4 < 4 * NT:
+                x_load(n + 4)
+            if n < 4 * NT:
+                x_turn(n)
                 xg[n] = ring_at("xg", [P, 2048], BF16, XG_OFF)
-            turn_copy(xb[n0], xg[n0], 0, nc.scalar.copy)
-            turn_copy(xb[n0], xg[n0], 1, nc.scalar.copy)
-            turn_copy(xb[n0 + 1], xg[n0 + 1], 0, nc.scalar.copy)
-            if n0 < HEAD_UNITS:
-                turn_copy(xb[n0 + 1], xg[n0 + 1], 1, nc.scalar.copy)
-                wa_tick(0, n0)
-                x_quant(n0)
-                wa_tick(0, n0 + 1)
-                x_quant(n0 + 1)
-            else:
-                x_quant(n0)
-                turn_copy(xb[n0 + 1], xg[n0 + 1], 1, nc.vector.tensor_copy)
-                if n0 == HEAD_UNITS:
-                    wa_tick(0, 8)
-                if h >= 7 and h % 2 == 1 and (h - 9) // 2 <= 8:
-                    wa_tick(1, (h - 9) // 2)
-                x_quant(n0 + 1)
+                turn_copy(xb[n], xg[n], 0, nc.scalar.copy)
+                if n < HEAD_UNITS or n % 2 == 0:
+                    turn_copy(xb[n], xg[n], 1, nc.scalar.copy)
+                else:
+                    turn_copy(xb[n], xg[n], 1, nc.vector.tensor_copy)
+            if n <= 8:
+                wa_tick(0, n)
+            if n >= 14 and n % 4 == 2 and (n - 18) // 4 <= 8:
+                wa_tick(1, (n - 18) // 4)
+            if n >= 1:
+                x_quant(n - 1)
             issued = 0
-            while h >= M_START and state["next_half"] <= h - 2 and issued < 2:
-                m_half(state["next_half"])
-                state["next_half"] = state["next_half"] + 1
+            while n >= M_START and state["next_part"] <= n - M_LAG and issued < 2:
+                m_part(state["next_part"])
+                state["next_part"] = state["next_part"] + 1
                 issued = issued + 1
-        while state["next_half"] < 2 * NT:
-            m_half(state["next_half"])
-            state["next_half"] = state["next_half"] + 1
+        while state["next_part"] < 4 * NT:
+            m_part(state["next_part"])
+            state["next_part"] = state["next_part"] + 1
 
         for j in range(1, NCH - 1):
             for t in range(8):
@@ -510,72 +503,78 @@ def tile_multiheadlatentattention_pa_l_kernel(tc, x, Wkv_a, kv_norm_w, Wkv_b, ou
                 nsc[b4] = st([P, 512], U8, "ns%d" % b4, XS0 + 512 * b4)
             nc.vector.quantize_mx(out=ncod[i][:].bitcast(FP8X4), scales=nsc[b4][4 * a : 128, :], in_=ngt[i][:])
 
-        reload(0)
-        for t in range(9):
-            now = t < 8
-            prev = t >= 1
-            if now:
-                bk = pair_cells(2 * t, LAST)
-            if t == 0:
-                reload(1)
-            if prev:
-                nbk[2 * t - 2] = turn_pe(nbt[2 * t - 2])
-                nbk[2 * t - 1] = turn_pe(nbt[2 * t - 1])
-            if now:
-                last_evac(t, bk)
-            if prev:
-                n_copy(2 * t - 2)
-                n_copy(2 * t - 1)
-            if now:
-                rstd_chain(t)
-            if prev:
-                n_quant(2 * t - 2)
-            if now:
-                scale(2 * t)
-            if prev:
-                n_quant(2 * t - 1)
-            if now:
-                scale(2 * t + 1)
-            if t + 2 < 8:
-                reload(t + 2)
+        def s2_cell(s, c):
+            w, i = divmod(c, NT)
+            dst = o_k if w == 0 else o_v
+            wbc, wbs = wb[s][w]
+            a, b4 = i % 4, i // 4
+            bk = acc_bank() if c % 8 in (0, 3, 6) else tp_bank()
+            for g in range(G2):
+                nc.tensor.matmul_mx(
+                    out=bk[:],
+                    lhsT=ncod[i][:, 128 * g : 128 * (g + 1)].bitcast(FP8X4),
+                    lhsT_scale=nsc[b4][4 * a : 128, 128 * g : 128 * (g + 1)],
+                    rhs=wbc[:, 512 * g : 512 * (g + 1)].bitcast(FP8X4),
+                    rhs_scale=wbs[:, 512 * g : 512 * (g + 1)],
+                    start=(g == 0),
+                    stop=(g == G2 - 1),
+                )
+            osb = ring("os", [P, 512], F32, OS0, 2048, 8)
+            if c % 2 == 0:
+                nc.scalar.copy(out=osb[:], in_=bk[:])
+                nc.scalar.dma_start(out=dst[128 * i : 128 * (i + 1), 512 * s : 512 * (s + 1)], in_=osb[:])
+            else:
+                nc.vector.tensor_copy(out=osb[:], in_=bk[:])
+                nc.sync.dma_start(out=dst[128 * i : 128 * (i + 1), 512 * s : 512 * (s + 1)], in_=osb[:])
+            if s < 3:
+                g, r = divmod(c, 8)
+                if r == 0:
+                    wb_copy(s + 1, g, 0, nc.vector.tensor_copy)
+                    wb_copy(s + 1, g, 1, nc.scalar.copy)
+                if r == 2:
+                    wb_quant(s + 1, g, 0)
+                if r == 3:
+                    wb_quant(s + 1, g, 1)
+                if r == 4:
+                    if g + 2 < 4:
+                        wb_load(s + 1, g + 2, 4)
+                    elif s + 2 < 4:
+                        wb_load(s + 2, g - 2, 4)
 
-        wb_load(1, 0, 4)
-        wb_load(1, 1, 4)
+        reload(0)
+        accl = {}
+        wc7, ws7 = wch[LAST]
+        for i in range(NT + N_LAG):
+            t, e = divmod(i, 2)
+            if i < NT:
+                if e == 0:
+                    accl[t] = acc_bank()
+                cell_part(accl[t][:, CW * e : CW * (e + 1)], i, wc7, ws7, CW, 0, G1)
+            if i == 1:
+                reload(1)
+            if i == NT - 1:
+                wb_load(1, 0, 4)
+                wb_load(1, 1, 4)
+            m = i - N_LAG
+            if m >= 0:
+                nbk[m] = turn_pe(nbt[m])
+            if i < NT and e == 1:
+                last_evac(t, accl[t])
+                rstd_chain(t)
+            if m >= 0:
+                n_copy(m)
+                n_quant(m)
+            if i < NT and e == 1:
+                scale(i - 1)
+            if 2 <= i <= NT and e == 0:
+                scale(i - 1)
+                if t + 1 < 8:
+                    reload(t + 1)
+            if i >= NT - 1:
+                for c in range(4 * (i - NT + 1), 4 * (i - NT + 2)):
+                    s2_cell(0, c)
+
         for s in range(4):
             for c in range(2 * NT):
-                w, i = divmod(c, NT)
-                dst = o_k if w == 0 else o_v
-                wbc, wbs = wb[s][w]
-                a, b4 = i % 4, i // 4
-                bk = acc_bank() if c % 8 in (0, 3, 6) else tp_bank()
-                for g in range(G2):
-                    nc.tensor.matmul_mx(
-                        out=bk[:],
-                        lhsT=ncod[i][:, 128 * g : 128 * (g + 1)].bitcast(FP8X4),
-                        lhsT_scale=nsc[b4][4 * a : 128, 128 * g : 128 * (g + 1)],
-                        rhs=wbc[:, 512 * g : 512 * (g + 1)].bitcast(FP8X4),
-                        rhs_scale=wbs[:, 512 * g : 512 * (g + 1)],
-                        start=(g == 0),
-                        stop=(g == G2 - 1),
-                    )
-                osb = ring("os", [P, 512], F32, OS0, 2048, 8)
-                if c % 2 == 0:
-                    nc.scalar.copy(out=osb[:], in_=bk[:])
-                    nc.scalar.dma_start(out=dst[128 * i : 128 * (i + 1), 512 * s : 512 * (s + 1)], in_=osb[:])
-                else:
-                    nc.vector.tensor_copy(out=osb[:], in_=bk[:])
-                    nc.sync.dma_start(out=dst[128 * i : 128 * (i + 1), 512 * s : 512 * (s + 1)], in_=osb[:])
-                if s < 3:
-                    g, r = divmod(c, 8)
-                    if r == 0:
-                        wb_copy(s + 1, g, 0, nc.vector.tensor_copy)
-                        wb_copy(s + 1, g, 1, nc.scalar.copy)
-                    if r == 2:
-                        wb_quant(s + 1, g, 0)
-                    if r == 3:
-                        wb_quant(s + 1, g, 1)
-                    if r == 4:
-                        if g + 2 < 4:
-                            wb_load(s + 1, g + 2, 4)
-                        elif s + 2 < 4:
-                            wb_load(s + 2, g - 2, 4)
+                if s > 0 or c >= 4 * (N_LAG + 1):
+                    s2_cell(s, c)

@@ -43,7 +43,8 @@ ID0 = GN0 + 4096
 SQ0 = ID0 + 512
 JK0 = SQ0 + 512
 SM0 = JK0 + 512
-XR_OFF = (XR0, XR0 + 4096, XR0 + 8192, RC0, RC0 + 4096, CF0)
+XR_OFF = (XR0, XR0 + 4096, XR0 + 8192, RC0)
+XO_OFF = (RC0 + 4096, CF0)
 XG_OFF = (XG0, XG0 + 4096, SF0)
 CB_OFF = (WR0, WR0 + 8192, XC0, XC0 + 8192)
 NB_OFF = (WR0 + 16384, WR0 + 20480)
@@ -54,6 +55,9 @@ WBC_OFF = (XR0, XC0 + 6 * 8192)
 OS0 = XC0 + 9 * 8192
 
 M_START = 12
+C1_TICK0 = 10
+C1_EVERY = 4
+SORT_FROM = 16
 M_LAG = 6
 N_LAG = 3
 HEAD_UNITS = 8
@@ -142,8 +146,35 @@ def tile_multiheadlatentattention_pa_l_kernel(tc, x, Wkv_a, kv_norm_w, Wkv_b, ou
             xr[n] = ring_at("xr", [P, 2048], BF16, XR_OFF)
             nc.sync.dma_start(out=xr[n][:], in_=xf[128 * i : 128 * (i + 1), 2048 * q : 2048 * (q + 1)])
 
+        xo = {}
+
+        def sort_words(dst, src, copy):
+            copy(
+                out=dst[:].bitcast(F32).rearrange("p (l u w) -> p l u w", l=4, u=2),
+                in_=src[:].bitcast(F32).rearrange("p (l w u) -> p l u w", l=4, u=2),
+            )
+
+        def turn_sorted(src):
+            words = src[:].bitcast(F32)
+            banks = []
+            for hb in range(2):
+                bk = tp_bank()
+                for lu in range(4):
+                    nc.tensor.transpose(
+                        bk[:, 128 * lu : 128 * (lu + 1)], words[:, 512 * hb + 128 * lu : 512 * hb + 128 * (lu + 1)], ident[:]
+                    )
+                banks.append(bk)
+            return banks
+
+        def x_sort(n):
+            xo[n] = ring_at("xo", [P, 2048], BF16, XO_OFF)
+            sort_words(xo[n], xr[n], nc.vector.tensor_copy)
+
         def x_turn(n):
-            xb[n] = turn_pe(xr[n])
+            if n < SORT_FROM:
+                xb[n] = turn_pe(xr[n])
+                return
+            xb[n] = turn_sorted(xo[n])
 
         def x_quant(n):
             i, q = divmod(n, 4)
@@ -342,69 +373,84 @@ def tile_multiheadlatentattention_pa_l_kernel(tc, x, Wkv_a, kv_norm_w, Wkv_b, ou
                 in_=wbgrp[w][:],
             )
 
-        state = {"next_part": 0}
-        acc0 = {}
+        nxt = {0: 0, 1: 0, "load": 4}
+        accm = {}
 
-        def m_part(k):
-            i, part = divmod(k, 4)
+        def m_part(j):
+            i, part = divmod(nxt[j], 4)
+            nxt[j] = nxt[j] + 1
             if i % 2 == 0 and part == 0:
-                acc0[i // 2] = acc_bank()
-            bk = acc0[i // 2]
-            wc, ws = wch[0]
+                accm[j] = acc_bank()
+            bk = accm[j]
+            wc, ws = wch[j]
             cell_part(bk[:, CW * (i % 2) : CW * (i % 2 + 1)], i, wc, ws, CW, 4 * part, 4 * part + 4)
             if i % 2 == 1 and part == 3:
-                evac_store(bk, i - 1, 0)
+                evac_store(bk, i - 1, j)
 
+        c1_ready = C1_TICK0 + 8 * C1_EVERY + 2
         x_load(0)
         x_load(1)
         wa_tick(0, -1)
         x_load(2)
         x_load(3)
         for n in range(4 * NT + 1):
-            if n + 4 < 4 * NT:
-                x_load(n + 4)
+            if SORT_FROM <= n + 1 < 4 * NT:
+                x_sort(n + 1)
             if n < 4 * NT:
                 x_turn(n)
+            while nxt["load"] < 4 * NT and nxt["load"] - len(XR_OFF) <= (n + 1 if n + 1 >= SORT_FROM else n):
+                x_load(nxt["load"])
+                nxt["load"] = nxt["load"] + 1
+            if n < 4 * NT:
                 xg[n] = ring_at("xg", [P, 2048], BF16, XG_OFF)
                 turn_copy(xb[n], xg[n], 0, nc.scalar.copy)
-                if n < HEAD_UNITS or n % 2 == 0:
-                    turn_copy(xb[n], xg[n], 1, nc.scalar.copy)
-                else:
-                    turn_copy(xb[n], xg[n], 1, nc.vector.tensor_copy)
+                turn_copy(xb[n], xg[n], 1, nc.scalar.copy)
             if n <= 8:
                 wa_tick(0, n)
-            if n >= 14 and n % 4 == 2 and (n - 18) // 4 <= 8:
-                wa_tick(1, (n - 18) // 4)
+            if n == C1_TICK0 - 1:
+                wa_tick(1, -1)
+            if n >= C1_TICK0 and (n - C1_TICK0) % C1_EVERY == 0 and (n - C1_TICK0) // C1_EVERY <= 8:
+                wa_tick(1, (n - C1_TICK0) // C1_EVERY)
             if n >= 1:
                 x_quant(n - 1)
-            issued = 0
-            while n >= M_START and state["next_part"] <= n - M_LAG and issued < 2:
-                m_part(state["next_part"])
-                state["next_part"] = state["next_part"] + 1
-                issued = issued + 1
-        while state["next_part"] < 4 * NT:
-            m_part(state["next_part"])
-            state["next_part"] = state["next_part"] + 1
+            if n >= M_START:
+                issued = 0
+                if nxt[0] <= n - M_LAG:
+                    m_part(0)
+                    issued = 1
+                if n >= c1_ready and nxt[1] <= n - M_LAG:
+                    m_part(1)
+                    issued = issued + 1
+                if issued < 2 and nxt[0] <= n - M_LAG:
+                    m_part(0)
+        while nxt[0] < 4 * NT:
+            m_part(0)
+        left = 0
+        while nxt[1] < 4 * NT:
+            m_part(1)
+            if left % 3 == 0 and left // 3 <= 9:
+                wa_tick(2, left // 3 - 1)
+            left = left + 1
 
-        for j in range(1, NCH - 1):
+        for j in range(2, NCH - 1):
             for t in range(8):
                 if t == 0:
                     wa_tick(j + 1, -1)
                 evac_store(pair_cells(2 * t, j), 2 * t, j)
-                if j == 4 and 1 <= t <= 4:
+                if j == 5 and 1 <= t <= 4:
                     rope_w_copy(t - 1)
                 wa_tick(j + 1, t)
                 if t == 7:
                     wa_tick(j + 1, 8)
-                if j == 1 and t == 0:
+                if j == 2 and t == 0:
                     nc.sync.dma_start(out=gain[:], in_=kv_norm_w.partition_broadcast(P))
                     rope_tables_pool()
-                if j == 3 and t == 0:
-                    rope_tables_finish()
                 if j == 4 and t == 0:
+                    rope_tables_finish()
+                if j == 5 and t == 0:
                     for q in range(4):
                         rope_w_load(q)
-                if j == 4 and 1 <= t <= 4:
+                if j == 5 and 1 <= t <= 4:
                     rope_w_quant(t - 1)
 
         rc = tabs["rc"]

@@ -58,6 +58,7 @@ M_START = 12
 C1_TICK0 = 10
 C1_EVERY = 4
 SORT_FROM = 16
+TICKS = ((0, 1), (2,), (3,), (4,), (5,), (6, 7), (8,), ())
 M_LAG = 6
 N_LAG = 3
 HEAD_UNITS = 8
@@ -278,11 +279,14 @@ def tile_multiheadlatentattention_pa_l_kernel(tc, x, Wkv_a, kv_norm_w, Wkv_b, ou
             tabs["tl"] = st([P, 8, 64], F32, "tl", s0 + 128 + 4096)
             nc.gpsimd.iota(pos_i[:], pattern=[[128, 8]], base=0, channel_multiplier=1)
             nc.vector.tensor_copy(out=pos[:], in_=pos_i[:])
-            for i in range(64):
+            tabs["pos"] = pos
+
+        def rope_turns(i0, i1):
+            for i in range(i0, i1):
                 parts = split3(pow(10000.0, -i / 64.0) / TWO_PI)
                 for key, c in zip(("th", "tm", "tl"), parts):
-                    nc.gpsimd.tensor_scalar(
-                        out=tabs[key][:, :, i], in0=pos[:], scalar1=c, scalar2=0.0, op0=ALU.mult, op1=ALU.add
+                    nc.vector.tensor_scalar(
+                        out=tabs[key][:, :, i], in0=tabs["pos"][:], scalar1=c, scalar2=0.0, op0=ALU.mult, op1=ALU.add
                     )
 
         def rope_tables_finish():
@@ -360,7 +364,7 @@ def tile_multiheadlatentattention_pa_l_kernel(tc, x, Wkv_a, kv_norm_w, Wkv_b, ou
             copy(out=wbgrp[w][:].rearrange("p (h d t) -> p h d t", h=4, t=4), in_=src[:, w])
 
         def wb_quant(s, g, w):
-            if g == 0 and w == 0:
+            if s not in wb:
                 base = WBC_OFF[s % 2]
                 wb[s] = []
                 for v in range(2):
@@ -431,20 +435,22 @@ def tile_multiheadlatentattention_pa_l_kernel(tc, x, Wkv_a, kv_norm_w, Wkv_b, ou
             if left % 3 == 0 and left // 3 <= 9:
                 wa_tick(2, left // 3 - 1)
             left = left + 1
+        wa_tick(3, -1)
 
         for j in range(2, NCH - 1):
             for t in range(8):
-                if t == 0:
-                    wa_tick(j + 1, -1)
                 evac_store(pair_cells(2 * t, j), 2 * t, j)
                 if j == 5 and 1 <= t <= 4:
                     rope_w_copy(t - 1)
-                wa_tick(j + 1, t)
-                if t == 7:
-                    wa_tick(j + 1, 8)
+                for s in TICKS[t]:
+                    wa_tick(j + 1, s)
+                if t == 7 and j + 2 < NCH:
+                    wa_tick(j + 2, -1)
                 if j == 2 and t == 0:
                     nc.sync.dma_start(out=gain[:], in_=kv_norm_w.partition_broadcast(P))
                     rope_tables_pool()
+                if j in (2, 3):
+                    rope_turns(4 * (8 * (j - 2) + t), 4 * (8 * (j - 2) + t) + 4)
                 if j == 4 and t == 0:
                     rope_tables_finish()
                 if j == 5 and t == 0:
@@ -453,6 +459,14 @@ def tile_multiheadlatentattention_pa_l_kernel(tc, x, Wkv_a, kv_norm_w, Wkv_b, ou
                 if j == 5 and 1 <= t <= 4:
                     rope_w_quant(t - 1)
 
+        cbs = {}
+        LAST = NCH - 1
+
+        def reload_tile(i):
+            cbs[i] = st([P, 2048], F32, "cb%d" % (i % 4), CB_OFF[i % 4])
+            nc.sync.dma_start(out=cbs[i][:, 0 : CW * LAST], in_=o_k[128 * i : 128 * (i + 1), 0 : CW * LAST])
+
+        reload_tile(0)
         rc = tabs["rc"]
         rs = tabs["rs"]
         cf = tabs["cf"]
@@ -463,8 +477,6 @@ def tile_multiheadlatentattention_pa_l_kernel(tc, x, Wkv_a, kv_norm_w, Wkv_b, ou
             bk = acc_bank()
             for e in range(4):
                 cell_part(bk[:, 128 * e : 128 * (e + 1)], 4 * gq + e, rc, rs, 128, 0, G1)
-            wb_copy(0, gq, 0, nc.vector.tensor_copy)
-            wb_copy(0, gq, 1, nc.scalar.copy)
             a0 = (4 * gq) % 8
             t1 = ring("cs", [P, 512], F32, CS0, 2048, 3)
             t2 = ring("cs", [P, 512], F32, CS0, 2048, 3)
@@ -481,25 +493,24 @@ def tile_multiheadlatentattention_pa_l_kernel(tc, x, Wkv_a, kv_norm_w, Wkv_b, ou
                 out=o_r[512 * gq : 512 * (gq + 1), :].rearrange("(t p) d -> p t d", p=P),
                 in_=t1[:].rearrange("p (t d) -> p t d", t=4),
             )
-            wb_quant(0, gq, 0)
+            wb_copy(0, gq, 1, nc.scalar.copy)
+            wb_copy(0, gq, 0, nc.vector.tensor_copy)
             wb_quant(0, gq, 1)
+            wb_quant(0, gq, 0)
             if gq + 2 < 4:
                 wb_load(0, gq + 2, 2)
 
-        cbs = {}
         rstd = {}
         nbt = {}
         nbk = {}
         ngt = {}
         ncod = {}
         nsc = {}
-        LAST = NCH - 1
 
         def reload(t):
-            for e in range(2):
-                i = 2 * t + e
-                cbs[i] = st([P, 2048], F32, "cb%d" % (i % 4), CB_OFF[i % 4])
-                nc.sync.dma_start(out=cbs[i][:, 0 : CW * LAST], in_=o_k[128 * i : 128 * (i + 1), 0 : CW * LAST])
+            for i in (2 * t, 2 * t + 1):
+                if i not in cbs:
+                    reload_tile(i)
 
         def small(tag, t, k):
             return st([P, 2], F32, "%s%d" % (tag, t % 2), SM0 + 64 * (1 + 2 * k + t % 2))
@@ -522,12 +533,16 @@ def tile_multiheadlatentattention_pa_l_kernel(tc, x, Wkv_a, kv_norm_w, Wkv_b, ou
                 axis=AX.X,
                 op=ALU.add,
             )
-            nc.gpsimd.tensor_scalar(out=ms[:], in0=ss[:], scalar1=1.0 / 2048.0, scalar2=EPS, op0=ALU.mult, op1=ALU.add)
+            nc.vector.tensor_scalar(out=ms[:], in0=ss[:], scalar1=1.0 / 2048.0, scalar2=EPS, op0=ALU.mult, op1=ALU.add)
             nc.gpsimd.tensor_tensor(out=y0[:], in0=ms[:], in1=neghalf[:], op=ALU.pow)
-            nc.gpsimd.tensor_tensor(out=aa[:], in0=y0[:], in1=y0[:], op=ALU.mult)
-            nc.gpsimd.tensor_tensor(out=aa[:], in0=aa[:], in1=ms[:], op=ALU.mult)
-            nc.gpsimd.tensor_scalar(out=aa[:], in0=aa[:], scalar1=-0.5, scalar2=1.5, op0=ALU.mult, op1=ALU.add)
-            nc.gpsimd.tensor_tensor(out=yy[:], in0=y0[:], in1=aa[:], op=ALU.mult)
+            rstd[t] = (ms, y0, aa, yy)
+
+        def rstd_newton(t):
+            ms, y0, aa, yy = rstd[t]
+            nc.vector.tensor_tensor(out=aa[:], in0=y0[:], in1=y0[:], op=ALU.mult)
+            nc.vector.tensor_tensor(out=aa[:], in0=aa[:], in1=ms[:], op=ALU.mult)
+            nc.vector.tensor_scalar(out=aa[:], in0=aa[:], scalar1=-0.5, scalar2=1.5, op0=ALU.mult, op1=ALU.add)
+            nc.vector.tensor_tensor(out=yy[:], in0=y0[:], in1=aa[:], op=ALU.mult)
             rstd[t] = yy
 
         def scale(i):
@@ -611,6 +626,7 @@ def tile_multiheadlatentattention_pa_l_kernel(tc, x, Wkv_a, kv_norm_w, Wkv_b, ou
                 n_copy(m)
                 n_quant(m)
             if i < NT and e == 1:
+                rstd_newton(t)
                 scale(i - 1)
             if 2 <= i <= NT and e == 0:
                 scale(i - 1)

from contextlib import ExitStack
import math

import concourse.masks as masks
import concourse.mybir as mybir

FLOPS = 2 * 2048 * 8192 * 2176 + 2 * 2048 * 2048 * 4096

F32 = mybir.dt.float32
BF16 = mybir.dt.bfloat16
U32 = mybir.dt.uint32
U8 = mybir.dt.uint8
I32 = mybir.dt.int32
FP8X4 = mybir.dt.float8_e4m3fn_x4
ALU = mybir.AluOpType
ACT = mybir.ActivationFunctionType
AX = mybir.AxisListType

P = 128
NT = 16
G1 = 16
G2 = 4
CW = 256
NCH = 8
EPS = 1.1920928955078125e-07
TWO_PI = 6.283185307179586

XC0 = 0
XS0 = XC0 + 16 * 8192
WC0 = XS0 + 16 * 512
WS0 = WC0 + 2 * 16384
WR0 = WS0 + 2 * 1024
RC0 = WR0 + 3 * 4096
RS0 = RC0 + 8192
CF0 = RS0 + 512
SF0 = CF0 + 4096
WG0 = SF0 + 4096
XR0 = WG0 + 2 * 4096
XG0 = XR0 + 3 * 4096
CS0 = XG0 + 2 * 4096
GN0 = CS0 + 3 * 2048
ID0 = GN0 + 4096
SQ0 = ID0 + 512
JK0 = SQ0 + 512
SM0 = JK0 + 512
XR_OFF = (XR0, XR0 + 4096, XR0 + 8192, RC0)
XO_OFF = (RC0 + 4096, CF0)
XG_OFF = (XG0, XG0 + 4096, SF0)
CB_OFF = (WR0, WR0 + 8192, XC0, XC0 + 8192)
NB_OFF = (WR0 + 16384, WR0 + 20480)
NG_OFF = (WR0 + 24576, CS0)
NC0 = XC0 + 2 * 8192
WBR_OFF = (WC0, WC0 + 8192, WC0 + 16384, WC0 + 24576)
WBC_OFF = (XR0, XC0 + 6 * 8192)
OS0 = XC0 + 9 * 8192

M_START = 12
C1_TICK0 = 10
C1_EVERY = 4
SORT_FROM = 16
TICKS = ((0, 1), (2,), (3,), (4,), (5,), (6, 7), (8,), ())
M_LAG = 6
N_LAG = 3
HEAD_UNITS = 8


def split3(c):
    e = -int(-math.log(c) / math.log(2.0)) - 1
    s1 = 2.0 ** (11 - e)
    hi = int(c * s1) / s1
    s2 = s1 * 4194304.0
    mid = int((c - hi) * s2) / s2
    lo = (c - hi) - mid
    return hi, mid, lo


def tile_multiheadlatentattention_pa_l_kernel(tc, x, Wkv_a, kv_norm_w, Wkv_b, out_0, out_1, out_2):
    nc = tc.nc
    xf = x.flatten_outer_dims()
    o_k = out_0.rearrange("b s h d -> (b s) (h d)")
    o_v = out_1.rearrange("b s h d -> (b s) (h d)")
    o_r = out_2.rearrange("b s o d -> (b s) (o d)")

    with ExitStack() as ctx:
        sb = ctx.enter_context(tc.tile_pool(name="sb", bufs=1))
        ps = ctx.enter_context(tc.psum_pool(name="ps", bufs=1))
        ctx.enter_context(tc.manual_schedule())
        cnt = {}

        def st(shape, dtype, tag, offset):
            return sb.tile(shape, dtype, name=tag, tag=tag, offset=offset, align_bytes=64)

        def ring_at(kind, shape, dtype, offsets):
            n = cnt.get(kind, 0) % len(offsets)
            cnt[kind] = cnt.get(kind, 0) + 1
            return st(shape, dtype, "%s%d" % (kind, n), offsets[n])

        def ring(kind, shape, dtype, base, size, depth):
            return ring_at(kind, shape, dtype, [base + size * n for n in range(depth)])

        def tp_bank():
            return ps.tile([P, 512], F32, name="tp", tag="tp", bufs=5)

        def acc_bank():
            return ps.tile([P, 512], F32, name="acc", tag="acc", bufs=3)

        ident = st([P, P], F32, "ident", ID0)
        masks.make_identity(nc, ident[:])
        ssq = st([P, NT * NCH], F32, "ssq", SQ0)
        junk = st([P, CW], BF16, "junk", JK0)
        neghalf = st([P, 2], F32, "neghalf", SM0)
        nc.vector.memset(neghalf[:], -0.5)
        gain = st([P, 2048], BF16, "gain", GN0)

        xc = {}
        xs = {}
        wch = {}

        def turn_pe(src):
            words = src[:].bitcast(F32)
            banks = []
            for hb in range(2):
                bk = tp_bank()
                for l in range(2):
                    for u in range(2):
                        lo = 256 * (2 * hb + l)
                        nc.tensor.transpose(
                            bk[:, 256 * l + 128 * u : 256 * l + 128 * (u + 1)],
                            words[:, lo + u : lo + 256 : 2],
                            ident[:],
                        )
                banks.append(bk)
            return banks

        def turn_copy(banks, dst, hb, copy):
            copy(
                out=dst[:].bitcast(F32)[:, 512 * hb : 512 * (hb + 1)].rearrange("p (l m u) -> p l m u", l=2, u=2),
                in_=banks[hb][:].rearrange("p (l u m) -> p l m u", l=2, u=2),
            )

        xr = {}
        xb = {}
        xg = {}

        def x_load(n):
            i, q = divmod(n, 4)
            xr[n] = ring_at("xr", [P, 2048], BF16, XR_OFF)
            nc.sync.dma_start(out=xr[n][:], in_=xf[128 * i : 128 * (i + 1), 2048 * q : 2048 * (q + 1)])

        xo = {}

        def sort_words(dst, src, copy):
            copy(
                out=dst[:].bitcast(F32).rearrange("p (l u w) -> p l u w", l=4, u=2),
                in_=src[:].bitcast(F32).rearrange("p (l w u) -> p l u w", l=4, u=2),
            )

        def turn_sorted(src):
            words = src[:].bitcast(F32)
            banks = []
            for hb in range(2):
                bk = tp_bank()
                for lu in range(4):
                    nc.tensor.transpose(
                        bk[:, 128 * lu : 128 * (lu + 1)], words[:, 512 * hb + 128 * lu : 512 * hb + 128 * (lu + 1)], ident[:]
                    )
                banks.append(bk)
            return banks

        def x_sort(n):
            xo[n] = ring_at("xo", [P, 2048], BF16, XO_OFF)
            sort_words(xo[n], xr[n], nc.vector.tensor_copy)

        def x_turn(n):
            if n < SORT_FROM:
                xb[n] = turn_pe(xr[n])
                return
            xb[n] = turn_sorted(xo[n])

        def x_quant(n):
            i, q = divmod(n, 4)
            if q == 0:
                xc[i] = st([P, G1 * 128], U32, "xc%d" % i, XC0 + 8192 * i)
                xs[i] = st([P, 512], U8, "xs%d" % i, XS0 + 512 * i)
            nc.vector.quantize_mx(
                out=xc[i][:, 512 * q : 512 * (q + 1)].bitcast(FP8X4),
                scales=xs[i][4 * q : 128, :],
                in_=xg[n][:],
            )

        wraw = {}
        wgrp = {}

        def wa_load(j, s):
            wraw[s] = ring("wr", [P, 2, 4, CW], BF16, WR0, 4096, 3)
            for l in range(2):
                g = 2 * s + l
                nc.sync.dma_start(
                    out=wraw[s][:, l, :, :],
                    in_=Wkv_a[512 * g : 512 * (g + 1), CW * j : CW * (j + 1)].rearrange("(p t) c -> p t c", t=4),
                )

        def wa_copy(j, s):
            wgrp[s] = ring("wg", [P, 2048], BF16, WG0, 4096, 2)
            nc.vector.tensor_copy(
                out=wgrp[s][:].rearrange("p (l c t) -> p l c t", l=2, t=4),
                in_=wraw[s][:].rearrange("p l t c -> p l c t"),
            )

        def wa_quant(j, s):
            if s == 0:
                wch[j] = (
                    st([P, G1 * CW], U32, "wc%d" % (j % 2), WC0 + 16384 * (j % 2)),
                    st([P, 4 * CW], U8, "ws%d" % (j % 2), WS0 + 1024 * (j % 2)),
                )
            wc, ws = wch[j]
            q, r = divmod(2 * s, 4)
            nc.vector.quantize_mx(
                out=wc[:, 512 * s : 512 * (s + 1)].bitcast(FP8X4),
                scales=ws[4 * q : 128, CW * r : CW * r + 512],
                in_=wgrp[s][:],
            )

        def wa_tick(j, s):
            if s == -1:
                wa_load(j, 0)
                wa_load(j, 1)
                return
            if s + 2 < 8:
                wa_load(j, s + 2)
            if s < 8:
                wa_copy(j, s)
            if s >= 1:
                wa_quant(j, s - 1)

        def cell_part(out_ap, i, wc, ws, width, g0, g1):
            for g in range(g0, g1):
                q, r = divmod(g, 4)
                nc.tensor.matmul_mx(
                    out=out_ap,
                    lhsT=xc[i][:, 128 * g : 128 * (g + 1)].bitcast(FP8X4),
                    lhsT_scale=xs[i][4 * q : 128, 128 * r : 128 * (r + 1)],
                    rhs=wc[:, width * g : width * (g + 1)].bitcast(FP8X4),
                    rhs_scale=ws[4 * q : 128, width * r : width * (r + 1)],
                    start=(g == 0),
                    stop=(g == G1 - 1),
                )

        def pair_cells(i, j):
            wc, ws = wch[j]
            bk = acc_bank()
            cell_part(bk[:, 0:CW], i, wc, ws, CW, 0, G1)
            cell_part(bk[:, CW : 2 * CW], i + 1, wc, ws, CW, 0, G1)
            return bk

        def square(src_ap, i, j):
            nc.scalar.activation(
                out=junk[:], in_=src_ap, func=ACT.Square, accum_out=ssq[:, NCH * i + j : NCH * i + j + 1]
            )

        def evac_store(bk, i, j):
            cs = ring("cs", [P, 512], F32, CS0, 2048, 3)
            nc.scalar.copy(out=cs[:], in_=bk[:])
            for e in range(2):
                square(cs[:, CW * e : CW * (e + 1)], i + e, j)
            nc.scalar.dma_start(
                out=o_k[128 * i : 128 * (i + 2), CW * j : CW * (j + 1)].rearrange("(t p) c -> p t c", p=P),
                in_=cs[:].rearrange("p (t c) -> p t c", t=2),
            )

        tabs = {}

        def rope_tables_pool():
            s0 = XR0
            pos_i = st([P, 8], I32, "pos_i", s0)
            pos = st([P, 8], F32, "pos", s0 + 64)
            tabs["th"] = st([P, 8, 64], F32, "th", s0 + 128)
            tabs["tm"] = st([P, 8, 64], F32, "tm", s0 + 128 + 2048)
            tabs["tl"] = st([P, 8, 64], F32, "tl", s0 + 128 + 4096)
            nc.gpsimd.iota(pos_i[:], pattern=[[128, 8]], base=0, channel_multiplier=1)
            nc.vector.tensor_copy(out=pos[:], in_=pos_i[:])
            tabs["pos"] = pos

        def rope_turns(i0, i1):
            for i in range(i0, i1):
                parts = split3(pow(10000.0, -i / 64.0) / TWO_PI)
                for key, c in zip(("th", "tm", "tl"), parts):
                    nc.vector.tensor_scalar(
                        out=tabs[key][:, :, i], in0=tabs["pos"][:], scalar1=c, scalar2=0.0, op0=ALU.mult, op1=ALU.add
                    )

        def rope_tables_finish():
            s0 = XR0
            ki = st([P, 512], I32, "ki", s0 + 128 + 6144)
            kf = st([P, 512], F32, "kf", s0 + 128 + 8192)
            fr = st([P, 2, 512], F32, "fr", s0 + 128 + 10240)
            zz = st([P, 1024], F32, "zz", s0 + 128 + 14336)
            thf = tabs["th"][:].rearrange("p a i -> p (a i)")
            nc.vector.tensor_copy(out=ki[:], in_=thf)
            nc.vector.tensor_copy(out=kf[:], in_=ki[:])
            nc.vector.tensor_tensor(out=fr[:, 0, :], in0=thf, in1=kf[:], op=ALU.subtract)
            for key in ("tm", "tl"):
                nc.vector.tensor_tensor(
                    out=fr[:, 0, :], in0=fr[:, 0, :], in1=tabs[key][:].rearrange("p a i -> p (a i)"), op=ALU.add
                )
            nc.vector.tensor_scalar_add(out=fr[:, 1, :], in0=fr[:, 0, :], scalar1=0.25)
            frf = fr[:].rearrange("p w n -> p (w n)")
            nc.vector.scalar_tensor_tensor(out=zz[:], in0=frf, scalar=0.5, in1=frf, op0=ALU.is_gt, op1=ALU.subtract)
            nc.vector.scalar_tensor_tensor(out=frf, in0=zz[:], scalar=0.5, in1=zz[:], op0=ALU.is_gt, op1=ALU.subtract)
            cf = st([P, 8, 64, 2], F32, "cf", CF0)
            sf = st([P, 8, 64, 2], F32, "sf", SF0)
            sin_in = fr[:, 0, :].rearrange("p (a i) -> p a i", a=8)
            cos_in = fr[:, 1, :].rearrange("p (a i) -> p a i", a=8)
            nc.scalar.activation(out=cf[:, :, :, 0], in_=cos_in, func=ACT.Sin, scale=TWO_PI)
            nc.scalar.activation(out=cf[:, :, :, 1], in_=cos_in, func=ACT.Sin, scale=TWO_PI)
            nc.scalar.activation(out=sf[:, :, :, 0], in_=sin_in, func=ACT.Sin, scale=-TWO_PI)
            nc.scalar.activation(out=sf[:, :, :, 1], in_=sin_in, func=ACT.Sin, scale=TWO_PI)
            tabs["cf"] = cf
            tabs["sf"] = sf

        rraw = {}
        rgrp = {}

        def rope_w_load(q):
            rraw[q] = st([P, 4, 4, 128], BF16, "rr%d" % q, XR0 + 4096 * q)
            for l in range(4):
                g = 4 * q + l
                nc.sync.dma_start(
                    out=rraw[q][:, l, :, :],
                    in_=Wkv_a[512 * g : 512 * (g + 1), 2048:2176].rearrange("(p t) c -> p t c", t=4),
                )

        def rope_w_copy(q):
            rgrp[q] = st([P, 2048], BF16, "rg", XG0 + 4096)
            nc.vector.tensor_copy(
                out=rgrp[q][:].rearrange("p (l c t) -> p l c t", l=4, t=4),
                in_=rraw[q][:].rearrange("p l t c -> p l c t"),
            )

        def rope_w_quant(q):
            if q == 0:
                tabs["rc"] = st([P, G1 * 128], U32, "rc", RC0)
                tabs["rs"] = st([P, 512], U8, "rs", RS0)
            nc.vector.quantize_mx(
                out=tabs["rc"][:, 512 * q : 512 * (q + 1)].bitcast(FP8X4),
                scales=tabs["rs"][4 * q : 128, :],
                in_=rgrp[q][:],
            )

        wb = {}
        wbraw = {}
        wbgrp = {}

        def wb_load(s, g, depth):
            wbraw[g] = ring_at("wbr", [P, 4, 1024], BF16, WBR_OFF[0:depth])
            nc.sync.dma_start(
                out=wbraw[g][:],
                in_=Wkv_b[512 * g : 512 * (g + 1), 1024 * s : 1024 * (s + 1)].rearrange("(p t) c -> p t c", t=4),
            )

        def wb_copy(s, g, w, copy):
            wbgrp[w] = ring("wg", [P, 2048], BF16, WG0, 4096, 2)
            src = wbraw[g][:].rearrange("p t (h w d) -> p w h d t", w=2, d=128)
            copy(out=wbgrp[w][:].rearrange("p (h d t) -> p h d t", h=4, t=4), in_=src[:, w])

        def wb_quant(s, g, w):
            if s not in wb:
                base = WBC_OFF[s % 2]
                wb[s] = []
                for v in range(2):
                    wbc_t = st([P, G2 * 512], U32, "wbc%d_%d" % (s % 2, v), base + 8192 * v)
                    wbs_t = st([P, G2 * 512], U8, "wbs%d_%d" % (s % 2, v), base + 16384 + 2048 * v)
                    wb[s].append((wbc_t, wbs_t))
            nc.vector.quantize_mx(
                out=wb[s][w][0][:, 512 * g : 512 * (g + 1)].bitcast(FP8X4),
                scales=wb[s][w][1][:, 512 * g : 512 * (g + 1)],
                in_=wbgrp[w][:],
            )

        nxt = {0: 0, 1: 0, "load": 4}
        accm = {}

        def m_part(j):
            i, part = divmod(nxt[j], 4)
            nxt[j] = nxt[j] + 1
            if i % 2 == 0 and part == 0:
                accm[j] = acc_bank()
            bk = accm[j]
            wc, ws = wch[j]
            cell_part(bk[:, CW * (i % 2) : CW * (i % 2 + 1)], i, wc, ws, CW, 4 * part, 4 * part + 4)
            if i % 2 == 1 and part == 3:
                evac_store(bk, i - 1, j)

        c1_ready = C1_TICK0 + 8 * C1_EVERY + 2
        x_load(0)
        x_load(1)
        wa_tick(0, -1)
        x_load(2)
        x_load(3)
        for n in range(4 * NT + 1):
            if SORT_FROM <= n + 1 < 4 * NT:
                x_sort(n + 1)
            if n < 4 * NT:
                x_turn(n)
            while nxt["load"] < 4 * NT and nxt["load"] - len(XR_OFF) <= (n + 1 if n + 1 >= SORT_FROM else n):
                x_load(nxt["load"])
                nxt["load"] = nxt["load"] + 1
            if n < 4 * NT:
                xg[n] = ring_at("xg", [P, 2048], BF16, XG_OFF)
                turn_copy(xb[n], xg[n], 0, nc.scalar.copy)
                turn_copy(xb[n], xg[n], 1, nc.scalar.copy)
            if n <= 8:
                wa_tick(0, n)
            if n == C1_TICK0 - 1:
                wa_tick(1, -1)
            if n >= C1_TICK0 and (n - C1_TICK0) % C1_EVERY == 0 and (n - C1_TICK0) // C1_EVERY <= 8:
                wa_tick(1, (n - C1_TICK0) // C1_EVERY)
            if n >= 1:
                x_quant(n - 1)
            if n >= M_START:
                issued = 0
                if nxt[0] <= n - M_LAG:
                    m_part(0)
                    issued = 1
                if n >= c1_ready and nxt[1] <= n - M_LAG:
                    m_part(1)
                    issued = issued + 1
                if issued < 2 and nxt[0] <= n - M_LAG:
                    m_part(0)
        while nxt[0] < 4 * NT:
            m_part(0)
        left = 0
        while nxt[1] < 4 * NT:
            m_part(1)
            if left % 3 == 0 and left // 3 <= 9:
                wa_tick(2, left // 3 - 1)
            left = left + 1
        wa_tick(3, -1)

        for j in range(2, NCH - 1):
            for t in range(8):
                evac_store(pair_cells(2 * t, j), 2 * t, j)
                if j == 5 and 1 <= t <= 4:
                    rope_w_copy(t - 1)
                for s in TICKS[t]:
                    wa_tick(j + 1, s)
                if t == 7 and j + 2 < NCH:
                    wa_tick(j + 2, -1)
                if j == 2 and t == 0:
                    nc.sync.dma_start(out=gain[:], in_=kv_norm_w.partition_broadcast(P))
                    rope_tables_pool()
                if j in (2, 3):
                    rope_turns(4 * (8 * (j - 2) + t), 4 * (8 * (j - 2) + t) + 4)
                if j == 4 and t == 0:
                    rope_tables_finish()
                if j == 5 and t == 0:
                    for q in range(4):
                        rope_w_load(q)
                if j == 5 and 1 <= t <= 4:
                    rope_w_quant(t - 1)

        cbs = {}
        LAST = NCH - 1

        def reload_tile(i):
            cbs[i] = st([P, 2048], F32, "cb%d" % (i % 4), CB_OFF[i % 4])
            nc.sync.dma_start(out=cbs[i][:, 0 : CW * LAST], in_=o_k[128 * i : 128 * (i + 1), 0 : CW * LAST])

        reload_tile(0)
        rc = tabs["rc"]
        rs = tabs["rs"]
        cf = tabs["cf"]
        sf = tabs["sf"]
        wb_load(0, 0, 2)
        wb_load(0, 1, 2)
        for gq in range(4):
            bk = acc_bank()
            for e in range(4):
                cell_part(bk[:, 128 * e : 128 * (e + 1)], 4 * gq + e, rc, rs, 128, 0, G1)
            a0 = (4 * gq) % 8
            t1 = ring("cs", [P, 512], F32, CS0, 2048, 3)
            t2 = ring("cs", [P, 512], F32, CS0, 2048, 3)
            nc.vector.tensor_tensor(
                out=t1[:], in0=bk[:], in1=cf[:, a0 : a0 + 4].rearrange("p a i e -> p (a i e)"), op=ALU.mult
            )
            bv = bk[:].rearrange("p (n e) -> p n e", e=2)
            sv = sf[:, a0 : a0 + 4].rearrange("p a i e -> p (a i) e")
            t2v = t2[:].rearrange("p (n e) -> p n e", e=2)
            nc.vector.tensor_tensor(out=t2v[:, :, 0], in0=bv[:, :, 1], in1=sv[:, :, 0], op=ALU.mult)
            nc.vector.tensor_tensor(out=t2v[:, :, 1], in0=bv[:, :, 0], in1=sv[:, :, 1], op=ALU.mult)
            nc.vector.tensor_tensor(out=t1[:], in0=t1[:], in1=t2[:], op=ALU.add)
            nc.sync.dma_start(
                out=o_r[512 * gq : 512 * (gq + 1), :].rearrange("(t p) d -> p t d", p=P),
                in_=t1[:].rearrange("p (t d) -> p t d", t=4),
            )
            wb_copy(0, gq, 1, nc.scalar.copy)
            wb_copy(0, gq, 0, nc.vector.tensor_copy)
            wb_quant(0, gq, 1)
            wb_quant(0, gq, 0)
            if gq + 2 < 4:
                wb_load(0, gq + 2, 2)

        rstd = {}
        nbt = {}
        nbk = {}
        ngt = {}
        ncod = {}
        nsc = {}

        def reload(t):
            for i in (2 * t, 2 * t + 1):
                if i not in cbs:
                    reload_tile(i)

        def small(tag, t, k):
            return st([P, 2], F32, "%s%d" % (tag, t % 2), SM0 + 64 * (1 + 2 * k + t % 2))

        def last_evac(t, bk):
            for e in range(2):
                nc.scalar.copy(out=cbs[2 * t + e][:, CW * LAST : CW * NCH], in_=bk[:, CW * e : CW * (e + 1)])
            for e in range(2):
                square(cbs[2 * t + e][:, CW * LAST : CW * NCH], 2 * t + e, LAST)

        def rstd_chain(t):
            ss = small("ss", t, 0)
            ms = small("ms", t, 1)
            y0 = small("y0", t, 2)
            aa = small("aa", t, 3)
            yy = small("yy", t, 4)
            nc.vector.tensor_reduce(
                out=ss[:],
                in_=ssq[:, 2 * NCH * t : 2 * NCH * (t + 1)].rearrange("p (e j) -> p e j", e=2),
                axis=AX.X,
                op=ALU.add,
            )
            nc.vector.tensor_scalar(out=ms[:], in0=ss[:], scalar1=1.0 / 2048.0, scalar2=EPS, op0=ALU.mult, op1=ALU.add)
            nc.gpsimd.tensor_tensor(out=y0[:], in0=ms[:], in1=neghalf[:], op=ALU.pow)
            rstd[t] = (ms, y0, aa, yy)

        def rstd_newton(t):
            ms, y0, aa, yy = rstd[t]
            nc.vector.tensor_tensor(out=aa[:], in0=y0[:], in1=y0[:], op=ALU.mult)
            nc.vector.tensor_tensor(out=aa[:], in0=aa[:], in1=ms[:], op=ALU.mult)
            nc.vector.tensor_scalar(out=aa[:], in0=aa[:], scalar1=-0.5, scalar2=1.5, op0=ALU.mult, op1=ALU.add)
            nc.vector.tensor_tensor(out=yy[:], in0=y0[:], in1=aa[:], op=ALU.mult)
            rstd[t] = yy

        def scale(i):
            nbt[i] = ring_at("nb", [P, 2048], BF16, NB_OFF)
            nc.vector.scalar_tensor_tensor(
                out=nbt[i][:], in0=cbs[i][:], scalar=rstd[i // 2][:, i % 2 : i % 2 + 1], in1=gain[:],
                op0=ALU.mult, op1=ALU.mult,
            )

        def n_copy(i):
            ngt[i] = ring_at("ng", [P, 2048], BF16, NG_OFF)
            turn_copy(nbk[i], ngt[i], 0, nc.scalar.copy)
            turn_copy(nbk[i], ngt[i], 1, nc.scalar.copy)

        def n_quant(i):
            a, b4 = i % 4, i // 4
            ncod[i] = st([P, G2 * 128], U32, "nc%d" % i, NC0 + 2048 * i)
            if a == 0:
                nsc[b4] = st([P, 512], U8, "ns%d" % b4, XS0 + 512 * b4)
            nc.vector.quantize_mx(out=ncod[i][:].bitcast(FP8X4), scales=nsc[b4][4 * a : 128, :], in_=ngt[i][:])

        def s2_cell(s, c):
            w, i = divmod(c, NT)
            dst = o_k if w == 0 else o_v
            wbc, wbs = wb[s][w]
            a, b4 = i % 4, i // 4
            bk = acc_bank() if c % 8 in (0, 3, 6) else tp_bank()
            for g in range(G2):
                nc.tensor.matmul_mx(
                    out=bk[:],
                    lhsT=ncod[i][:, 128 * g : 128 * (g + 1)].bitcast(FP8X4),
                    lhsT_scale=nsc[b4][4 * a : 128, 128 * g : 128 * (g + 1)],
                    rhs=wbc[:, 512 * g : 512 * (g + 1)].bitcast(FP8X4),
                    rhs_scale=wbs[:, 512 * g : 512 * (g + 1)],
                    start=(g == 0),
                    stop=(g == G2 - 1),
                )
            osb = ring("os", [P, 512], F32, OS0, 2048, 8)
            if c % 2 == 0:
                nc.scalar.copy(out=osb[:], in_=bk[:])
                nc.scalar.dma_start(out=dst[128 * i : 128 * (i + 1), 512 * s : 512 * (s + 1)], in_=osb[:])
            else:
                nc.vector.tensor_copy(out=osb[:], in_=bk[:])
                nc.sync.dma_start(out=dst[128 * i : 128 * (i + 1), 512 * s : 512 * (s + 1)], in_=osb[:])
            if s < 3:
                g, r = divmod(c, 8)
                if r == 0:
                    wb_copy(s + 1, g, 0, nc.vector.tensor_copy)
                    wb_copy(s + 1, g, 1, nc.scalar.copy)
                if r == 2:
                    wb_quant(s + 1, g, 0)
                if r == 3:
                    wb_quant(s + 1, g, 1)
                if r == 4:
                    if g + 2 < 4:
                        wb_load(s + 1, g + 2, 4)
                    elif s + 2 < 4:
                        wb_load(s + 2, g - 2, 4)

        reload(0)
        accl = {}
        wc7, ws7 = wch[LAST]
        for i in range(NT + N_LAG):
            t, e = divmod(i, 2)
            if i < NT:
                if e == 0:
                    accl[t] = acc_bank()
                cell_part(accl[t][:, CW * e : CW * (e + 1)], i, wc7, ws7, CW, 0, G1)
            if i == 1:
                reload(1)
            if i == NT - 1:
                wb_load(1, 0, 4)
                wb_load(1, 1, 4)
            m = i - N_LAG
            if m >= 0:
                nbk[m] = turn_pe(nbt[m])
            if i < NT and e == 1:
                last_evac(t, accl[t])
                rstd_chain(t)
            if m >= 0:
                n_copy(m)
                n_quant(m)
            if i < NT and e == 1:
                rstd_newton(t)
                scale(i - 1)
            if 2 <= i <= NT and e == 0:
                scale(i - 1)
                if t + 1 < 8:
                    reload(t + 1)
            if i >= NT - 1:
                for c in range(4 * (i - NT + 1), 4 * (i - NT + 2)):
                    s2_cell(0, c)

        for s in range(4):
            for c in range(2 * NT):
                if s > 0 or c >= 4 * (N_LAG + 1):
                    s2_cell(s, c)
